import numpy as np
import ml_dtypes


def mxq(x, axis, fmt="e4m3"):
    dtype, down = {"e4m3": (ml_dtypes.float8_e4m3fn, 7), "e5m2": (ml_dtypes.float8_e5m2, 14)}[fmt]
    v = np.moveaxis(np.asarray(x, np.float32).astype(ml_dtypes.bfloat16).astype(np.float64), axis, -1)
    blocks = v.reshape(v.shape[:-1] + (-1, 32))
    amax = np.abs(blocks).max(-1, keepdims=True)
    byte = np.maximum(np.where(amax > 0, np.frexp(amax)[1] - 1 + 127, 0) - down, 1)
    scale = np.exp2(byte - 127.0)
    codes = (blocks / scale).astype(np.float32).astype(dtype).astype(np.float64)
    return np.moveaxis((codes * scale).reshape(v.shape), -1, axis)


WIDE = False


def mx_kscale(k):
    if not WIDE:
        return np.ones(k)
    levels = np.array([10, -10, 5, -5, 0])
    if k % 512:
        return np.exp2(np.random.permutation(np.resize(levels, k // 32))).repeat(32)
    a = np.empty((k // 512, 16))
    for p in range(k // 512):
        a[p, :8] = np.random.permutation(np.resize(levels, 8))
        for g in range(8):
            far = levels[np.abs(levels - a[p, g]) >= 10]
            a[p, g + 8] = far[np.random.randint(len(far))]
    return np.exp2(a.ravel()).repeat(32)


BF16 = ml_dtypes.bfloat16


def bf(x):
    return np.asarray(x, np.float32).astype(BF16)


def f64(x):
    return np.asarray(x).astype(np.float64)


B, S, N, D = 4, 128, 16384, 512


def setup_inputs():
    s = mx_kscale(N)
    return {"input_numeric": bf(np.random.standard_normal((B, S, 1))),
            "proj_w": bf(np.random.standard_normal((N, 1))),
            "proj_b": bf(np.random.standard_normal(N) + np.log(s)),
            "emb_table": bf(np.random.standard_normal((N, D)) * 0.15 * np.sqrt(N) * np.mean(s) / s[:, None])}


def reference(input_numeric, proj_w, proj_b, emb_table):
    logits = f64(input_numeric) * f64(proj_w)[:, 0] + f64(proj_b)
    e = np.exp(logits - logits.max(-1, keepdims=True))
    weights = e / e.sum(-1, keepdims=True)
    return mxq(weights, 2, "e4m3") @ mxq(f64(emb_table), 0, "e4m3")

@@ -1,0 +1,391 @@
+from contextlib import ExitStack
+
+import concourse.mybir as mybir
+from concourse.masks import make_identity
+
+F32 = mybir.dt.float32
+BF16 = mybir.dt.bfloat16
+U32 = mybir.dt.uint32
+U8 = mybir.dt.uint8
+FP8X4 = mybir.dt.float8_e4m3fn_x4
+ALU = mybir.AluOpType
+ACT = mybir.ActivationFunctionType
+AXIS = mybir.AxisListType
+
+P = 128
+BATCHES = 4
+VOCAB = 16384
+DIM = 512
+PACK = 4
+K_PASS = P * PACK
+PASSES = VOCAB // K_PASS
+CHUNK = 2048
+CHUNKS = VOCAB // CHUNK
+CHUNK_PASSES = CHUNK // K_PASS
+TOTAL = BATCHES * CHUNKS
+BANK = 512
+CHUNK_BANKS = CHUNK // BANK
+BANK_TILES = 8
+SPREAD_BANKS = CHUNK // (BANK_TILES * P)
+BANK_PASSES = 2
+PLANES = 4
+PLANE_ROWS = 4
+RUN = 4
+TENSOR_EVERY = 3
+TENSOR_CHUNKS = (CHUNKS + TENSOR_EVERY - 1) // TENSOR_EVERY
+VECTOR_CHUNKS = CHUNKS - TENSOR_CHUNKS
+ONES_PARTITION = 32
+EXP_BUFS = CHUNKS + 2
+TABLE_AHEAD = 2
+TABLE_LAG = 2
+NORMALISE_LAG = CHUNKS
+REGROUP_LAG = NORMALISE_LAG + 1
+MULTIPLY_LAG = NORMALISE_LAG + 2
+
+FLOPS = 2 * BATCHES * P * VOCAB * DIM
+
+
+def tile_softembedding_k_kernel(tc, input_numeric, proj_w, proj_b, emb_table, out):
+    nc = tc.nc
+    with ExitStack() as ctx:
+        keep = ctx.enter_context(tc.tile_pool(name="keep", bufs=1))
+        exp_pool = ctx.enter_context(tc.tile_pool(name="exp_pool", bufs=EXP_BUFS))
+        stats = ctx.enter_context(tc.tile_pool(name="stats", bufs=2))
+        psum_logit = ctx.enter_context(tc.psum_pool(name="psum_logit", bufs=CHUNK_BANKS))
+        psum_turn = ctx.enter_context(tc.psum_pool(name="psum_turn", bufs=3))
+        psum_out = ctx.enter_context(tc.psum_pool(name="psum_out", bufs=1))
+
+        identity = keep.tile([P, P], F32)
+        make_identity(nc, identity[:])
+        identity_bf = keep.tile([P, P], BF16)
+        make_identity(nc, identity_bf[:])
+
+        x_bf = keep.tile([P, BATCHES], BF16)
+        with nc.allow_non_contiguous_dma(reason="512 scalars, one token to a partition"):
+            nc.sync.dma_start(out=x_bf[:], in_=input_numeric.rearrange("b s o -> s (b o)"))
+        x_col = keep.tile([P, BATCHES], F32)
+        nc.vector.tensor_copy(out=x_col[:], in_=x_bf[:])
+
+        w_all = keep.tile([P, VECTOR_CHUNKS * CHUNK], BF16)
+        b_all = keep.tile([P, VECTOR_CHUNKS * CHUNK], BF16)
+        proj_loaded = keep.tile([P, 2, P], BF16)
+        nc.sync.dma_start(out=proj_loaded[:, 0, :], in_=proj_w.rearrange("(a p) o -> a (p o)", p=P))
+        nc.sync.dma_start(out=proj_loaded[:, 1, :], in_=proj_b.rearrange("(a p) -> a p", p=P))
+        proj_turned = psum_out.tile([P, 2, P], BF16, tag="row_acc")
+        nc.tensor.transpose(proj_turned[:, 0, :], proj_loaded[:, 0, :], identity_bf[:])
+        nc.tensor.transpose(proj_turned[:, 1, :], proj_loaded[:, 1, :], identity_bf[:])
+        proj_cols = keep.tile([P, 2, P], BF16)
+        nc.vector.tensor_copy(out=proj_cols[:], in_=proj_turned[:])
+
+        x_pair = keep.tile([P, BATCHES, P], BF16)
+        nc.vector.memset(x_pair[:], 0.0)
+        nc.vector.memset(x_pair[ONES_PARTITION : ONES_PARTITION + 1, :, :], 1.0)
+        nc.sync.dma_start(out=x_pair[0:1, :, :], in_=input_numeric.rearrange("b s o -> o b s"))
+        proj_pair = keep.tile([P, TENSOR_CHUNKS, CHUNK], BF16)
+        nc.vector.memset(proj_pair[:], 0.0)
+        for i in range(TENSOR_CHUNKS):
+            cols = slice(i * TENSOR_EVERY * CHUNK, (i * TENSOR_EVERY + 1) * CHUNK)
+            nc.sync.dma_start(out=proj_pair[0:1, i, :], in_=proj_w[cols, :].rearrange("n o -> o n"))
+            nc.sync.dma_start(
+                out=proj_pair[ONES_PARTITION : ONES_PARTITION + 1, i, :], in_=proj_b[cols].unsqueeze(0)
+            )
+
+        def vector_slot(j):
+            return j - j // TENSOR_EVERY - 1
+
+        table_codes = keep.tile([P, PASSES, DIM], U32, align_bytes=64)
+        table_scales = keep.tile([P, PASSES // PLANES, DIM], U8, align_bytes=64)
+
+        def table_plane(g):
+            return table_scales[PLANE_ROWS * (g % PLANES) : P, g // PLANES, :]
+
+        spread_banks = {}
+
+        def spread_projection(j, which):
+            for half in range(SPREAD_BANKS):
+                spread_bank = psum_turn.tile([P, BANK_TILES, P], BF16, tag="turn_bank")
+                for i in range(BANK_TILES):
+                    a = (SPREAD_BANKS * j + half) * BANK_TILES + i
+                    nc.tensor.transpose(
+                        spread_bank[:, i, :],
+                        proj_cols[:, which, a : a + 1].to_broadcast([P, P]),
+                        identity_bf[:],
+                    )
+                spread_banks[(j, which, half)] = spread_bank
+
+        def collect_projection(j, which):
+            target = b_all if which else w_all
+            for half in range(SPREAD_BANKS):
+                first = (SPREAD_BANKS * vector_slot(j) + half) * BANK_TILES * P
+                nc.scalar.copy(
+                    out=target[:, first : first + BANK_TILES * P],
+                    in_=spread_banks[(j, which, half)][:].rearrange("p i n -> p (i n)"),
+                )
+
+        table_rows = {}
+        table_grouped = {}
+
+        def load_table(stage, g):
+            pass_rows = stage.tile([P, PACK, DIM], BF16, bufs=TABLE_AHEAD + 1)
+            nc.sync.dma_start(
+                out=pass_rows[:],
+                in_=emb_table[g * K_PASS : (g + 1) * K_PASS, :].rearrange("(p t) d -> p t d", t=PACK),
+            )
+            table_rows[g] = pass_rows
+
+        def regroup_table(stage, g):
+            pass_grouped = stage.tile([P, DIM, PACK], BF16, align_bytes=64, bufs=TABLE_LAG + 2)
+            dst = pass_grouped[:].rearrange("p (r i) t -> p r t i", i=RUN)
+            src = table_rows[g][:].rearrange("p t (r i) -> p r t i", i=RUN)
+            if g % 2 == 0:
+                nc.vector.tensor_copy(out=dst, in_=src)
+            else:
+                nc.scalar.copy(out=dst, in_=src)
+            table_grouped[g] = pass_grouped
+
+        def quantise_table(g):
+            nc.vector.quantize_mx(
+                out=table_codes[:, g, :].bitcast(FP8X4),
+                scales=table_plane(g),
+                in_=table_grouped[g][:].rearrange("p d t -> p (d t)"),
+            )
+
+        exps = {}
+        logit_banks = {}
+        neg_max = {}
+        part_sum = {}
+        neg_top = {}
+        chunk_scale = {}
+
+        def logits(k):
+            b, j = divmod(k, CHUNKS)
+            if j == 0:
+                row_neg_max = stats.tile([P, CHUNKS], F32)
+                row_part_sum = stats.tile([P, CHUNKS, CHUNK_BANKS], F32)
+                nc.vector.memset(row_part_sum[:], 0.0)
+                neg_max[b] = row_neg_max
+                part_sum[b] = row_part_sum
+            chunk = exp_pool.tile([P, CHUNK], F32)
+            exps[k] = chunk
+            if j % TENSOR_EVERY == 0:
+                logit_banks[k] = []
+                for bank_no in range(CHUNK_BANKS):
+                    logit_bank = psum_logit.tile([P, BANK], F32)
+                    nc.tensor.matmul(
+                        out=logit_bank[:],
+                        lhsT=x_pair[:, b, :],
+                        rhs=proj_pair[:, j // TENSOR_EVERY, bank_no * BANK : (bank_no + 1) * BANK],
+                        start=True,
+                        stop=True,
+                    )
+                    logit_banks[k].append(logit_bank)
+            else:
+                cols = slice(vector_slot(j) * CHUNK, (vector_slot(j) + 1) * CHUNK)
+                nc.vector.scalar_tensor_tensor(
+                    out=chunk[:],
+                    in0=w_all[:, cols],
+                    scalar=x_col[:, b : b + 1],
+                    in1=b_all[:, cols],
+                    op0=ALU.mult,
+                    op1=ALU.add,
+                )
+
+        def maximum(k):
+            b, j = divmod(k, CHUNKS)
+            if j % TENSOR_EVERY == 0:
+                bank_neg_max = stats.tile([P, CHUNK_BANKS], F32)
+                for bank_no in range(CHUNK_BANKS):
+                    nc.vector.tensor_reduce(
+                        out=bank_neg_max[:, bank_no : bank_no + 1],
+                        in_=logit_banks[k][bank_no][:],
+                        axis=AXIS.X,
+                        op=ALU.max,
+                        negate=True,
+                    )
+                nc.vector.tensor_reduce(
+                    out=neg_max[b][:, j : j + 1], in_=bank_neg_max[:], axis=AXIS.X, op=ALU.min
+                )
+            else:
+                nc.vector.tensor_reduce(
+                    out=neg_max[b][:, j : j + 1], in_=exps[k][:], axis=AXIS.X, op=ALU.max, negate=True
+                )
+
+        def exponentials(k):
+            b, j = divmod(k, CHUNKS)
+            if j % TENSOR_EVERY == 0:
+                for bank_no in range(CHUNK_BANKS):
+                    nc.scalar.activation(
+                        out=exps[k][:, bank_no * BANK : (bank_no + 1) * BANK],
+                        in_=logit_banks[k][bank_no][:],
+                        func=ACT.Exp,
+                        bias=neg_max[b][:, j : j + 1],
+                        scale=1.0,
+                        accum_out=part_sum[b][:, j, bank_no : bank_no + 1],
+                    )
+            else:
+                nc.scalar.activation(
+                    out=exps[k][:],
+                    in_=exps[k][:],
+                    func=ACT.Exp,
+                    bias=neg_max[b][:, j : j + 1],
+                    scale=1.0,
+                    accum_out=part_sum[b][:, j, 0:1],
+                )
+
+        def row_top(b):
+            top = stats.tile([P, 1], F32)
+            nc.vector.tensor_reduce(out=top[:], in_=neg_max[b][:], axis=AXIS.X, op=ALU.min)
+            neg_top[b] = top
+
+        def row_scales(b):
+            factor = stats.tile([P, CHUNKS], F32)
+            nc.scalar.activation(
+                out=factor[:], in_=neg_max[b][:], func=ACT.Exp, bias=neg_top[b][:, 0:1], scale=-1.0
+            )
+            chunk_sum = stats.tile([P, CHUNKS], F32)
+            nc.vector.tensor_reduce(out=chunk_sum[:], in_=part_sum[b][:], axis=AXIS.X, op=ALU.add)
+            weighted = stats.tile([P, CHUNKS], F32)
+            nc.vector.tensor_tensor(out=weighted[:], in0=factor[:], in1=chunk_sum[:], op=ALU.mult)
+            total = stats.tile([P, 1], F32)
+            nc.vector.tensor_reduce(out=total[:], in_=weighted[:], axis=AXIS.X, op=ALU.add)
+            inv_total = stats.tile([P, 1], F32)
+            nc.vector.reciprocal(out=inv_total[:], in_=total[:])
+            row_chunk_scale = stats.tile([P, CHUNKS], F32)
+            nc.vector.tensor_scalar(
+                out=row_chunk_scale[:], in0=factor[:], scalar1=inv_total[:, 0:1], scalar2=None, op0=ALU.mult
+            )
+            chunk_scale[b] = row_chunk_scale
+
+        weights = {}
+        turned = {}
+        weight_grouped = {}
+        weight_codes = {}
+        weight_scales = {}
+        acc = {}
+
+        def normalise(stage, k, on_scalar):
+            b, j = divmod(k, CHUNKS)
+            chunk_weights = stage.tile([P, CHUNK], BF16)
+            if on_scalar:
+                nc.scalar.activation(
+                    out=chunk_weights[:], in_=exps[k][:], func=ACT.Copy, scale=chunk_scale[b][:, j : j + 1]
+                )
+            else:
+                nc.vector.tensor_scalar(
+                    out=chunk_weights[:],
+                    in0=exps[k][:],
+                    scalar1=chunk_scale[b][:, j : j + 1],
+                    scalar2=None,
+                    op0=ALU.mult,
+                )
+            weights[k] = chunk_weights
+
+        def turn(k):
+            words = weights[k][:].bitcast(F32)
+            turned[k] = []
+            for half in range(CHUNK_PASSES // BANK_PASSES):
+                turned_bank = psum_turn.tile([P, BANK_PASSES, 2, P], F32, tag="turn_bank")
+                for c in range(BANK_PASSES):
+                    for u in range(2):
+                        first = (BANK_PASSES * half + c) * 2 * P
+                        nc.tensor.transpose(
+                            turned_bank[:, c, u, :], words[:, first + u : first + 2 * P : 2], identity[:]
+                        )
+                turned[k].append(turned_bank)
+
+        def regroup(stage, k):
+            chunk_grouped = stage.tile([P, CHUNK_PASSES, P, PACK], BF16, align_bytes=64)
+            grouped_words = chunk_grouped[:].bitcast(F32)
+            for half in range(CHUNK_PASSES // BANK_PASSES):
+                nc.scalar.copy(
+                    out=grouped_words[:, BANK_PASSES * half : BANK_PASSES * (half + 1), :, :],
+                    in_=turned[k][half][:].rearrange("p c u s -> p c s u"),
+                )
+            weight_grouped[k] = chunk_grouped
+
+        def quantise(stage, k):
+            chunk_codes = stage.tile([P, CHUNK_PASSES * P], U32, align_bytes=64)
+            chunk_planes = stage.tile([P, CHUNK_PASSES * P], U8, align_bytes=64)
+            nc.vector.quantize_mx(
+                out=chunk_codes[:].bitcast(FP8X4),
+                scales=chunk_planes[:],
+                in_=weight_grouped[k][:].rearrange("p c s t -> p (c s t)"),
+            )
+            weight_codes[k] = chunk_codes
+            weight_scales[k] = chunk_planes
+
+        def multiply(k):
+            b, j = divmod(k, CHUNKS)
+            if j == 0:
+                row_acc = psum_out.tile([P, DIM], F32)
+                acc[b] = row_acc
+            for c in range(CHUNK_PASSES):
+                g = j * CHUNK_PASSES + c
+                tokens = slice(c * P, (c + 1) * P)
+                nc.tensor.matmul_mx(
+                    out=acc[b][:],
+                    lhsT=weight_codes[k][:, tokens].bitcast(FP8X4),
+                    lhsT_scale=weight_scales[k][:, tokens],
+                    rhs=table_codes[:, g, :].bitcast(FP8X4),
+                    rhs_scale=table_plane(g),
+                    start=(g == 0),
+                    stop=(g == PASSES - 1),
+                )
+
+        def store(stage, b):
+            result = stage.tile([P, DIM], F32)
+            nc.scalar.copy(out=result[:], in_=acc[b][:])
+            nc.sync.dma_start(out=out[b], in_=result[:])
+
+
+        with tc.tile_pool(name="table_stage", bufs=1) as table_stage:
+            for g in range(TABLE_AHEAD):
+                load_table(table_stage, g)
+            for k in range(CHUNKS):
+                spread_next = k + 1 < CHUNKS and (k + 1) % TENSOR_EVERY != 0
+                for quarter in range(CHUNK_PASSES):
+                    g = k * CHUNK_PASSES + quarter
+                    if g + TABLE_AHEAD < PASSES:
+                        load_table(table_stage, g + TABLE_AHEAD)
+                    regroup_table(table_stage, g)
+                    if g >= TABLE_LAG:
+                        quantise_table(g - TABLE_LAG)
+                    if quarter == 0:
+                        logits(k)
+                        if k >= 1:
+                            exponentials(k - 1)
+                    if quarter == 1:
+                        maximum(k)
+                    if quarter < 2 and spread_next:
+                        spread_projection(k + 1, quarter)
+                    if quarter >= 2 and spread_next:
+                        collect_projection(k + 1, quarter - 2)
+            for g in range(PASSES - TABLE_LAG, PASSES):
+                quantise_table(g)
+
+        with tc.tile_pool(name="weight_stage", bufs=2, reuse_waits="tile") as weight_stage:
+            for k in range(CHUNKS, TOTAL + MULTIPLY_LAG):
+                row_ends = k % CHUNKS == 0 and k <= TOTAL
+                if row_ends:
+                    row_top(k // CHUNKS - 1)
+                if k < TOTAL:
+                    logits(k)
+                    maximum(k)
+                on_scalar = k < TOTAL and k % 2 == 1
+                if k - NORMALISE_LAG < TOTAL and on_scalar:
+                    normalise(weight_stage, k - NORMALISE_LAG, True)
+                    turn(k - NORMALISE_LAG)
+                if k - 1 < TOTAL:
+                    exponentials(k - 1)
+                if row_ends:
+                    row_scales(k // CHUNKS - 1)
+                if k - NORMALISE_LAG < TOTAL and not on_scalar:
+                    normalise(weight_stage, k - NORMALISE_LAG, False)
+                    turn(k - NORMALISE_LAG)
+                if 0 <= k - REGROUP_LAG < TOTAL:
+                    regroup(weight_stage, k - REGROUP_LAG)
+                if 0 <= k - MULTIPLY_LAG:
+                    quantise(weight_stage, k - MULTIPLY_LAG)
+                    multiply(k - MULTIPLY_LAG)
+                    if (k - MULTIPLY_LAG) % CHUNKS == CHUNKS - 1:
+                        store(weight_stage, (k - MULTIPLY_LAG) // CHUNKS)

@@ -19,28 +19,28 @@ DIM = 512
 PACK = 4
 K_PASS = P * PACK
 PASSES = VOCAB // K_PASS
+SLICE = 512
+SLICES = VOCAB // SLICE
+TOTAL_SLICES = BATCHES * SLICES
+COLS = SLICE // P
 CHUNK = 2048
 CHUNKS = VOCAB // CHUNK
 CHUNK_PASSES = CHUNK // K_PASS
-TOTAL = BATCHES * CHUNKS
-BANK = 512
-CHUNK_BANKS = CHUNK // BANK
-BANK_TILES = 8
-SPREAD_BANKS = CHUNK // (BANK_TILES * P)
+CHUNK_SLICES = CHUNK // SLICE
+TOTAL_CHUNKS = BATCHES * CHUNKS
 BANK_PASSES = 2
 PLANES = 4
 PLANE_ROWS = 4
 RUN = 4
-TENSOR_EVERY = 3
-TENSOR_CHUNKS = (CHUNKS + TENSOR_EVERY - 1) // TENSOR_EVERY
-VECTOR_CHUNKS = CHUNKS - TENSOR_CHUNKS
+TENSOR_SHARE = 3
+TENSOR_OF = 8
+TENSOR_RESIDUES = [i for i in range(TENSOR_OF) if TENSOR_SHARE * i % TENSOR_OF < TENSOR_SHARE]
 ONES_PARTITION = 32
 EXP_BUFS = CHUNKS + 2
 TABLE_AHEAD = 2
 TABLE_LAG = 2
-NORMALISE_LAG = CHUNKS
-REGROUP_LAG = NORMALISE_LAG + 1
-MULTIPLY_LAG = NORMALISE_LAG + 2
+EXP_LAG = 2
+NORMALISE_LAG = SLICES + EXP_LAG
 
 FLOPS = 2 * BATCHES * P * VOCAB * DIM
 
@@ -50,77 +50,54 @@ def tile_softembedding_k_kernel(tc, input_numeric, proj_w, proj_b, emb_table, ou
     with ExitStack() as ctx:
         keep = ctx.enter_context(tc.tile_pool(name="keep", bufs=1))
         exp_pool = ctx.enter_context(tc.tile_pool(name="exp_pool", bufs=EXP_BUFS))
+        logit_cols = ctx.enter_context(tc.tile_pool(name="logit_cols", bufs=3))
         stats = ctx.enter_context(tc.tile_pool(name="stats", bufs=2))
-        psum_logit = ctx.enter_context(tc.psum_pool(name="psum_logit", bufs=CHUNK_BANKS))
+        psum_logit = ctx.enter_context(tc.psum_pool(name="psum_logit", bufs=4))
         psum_turn = ctx.enter_context(tc.psum_pool(name="psum_turn", bufs=3))
         psum_out = ctx.enter_context(tc.psum_pool(name="psum_out", bufs=1))
 
-        identity = keep.tile([P, P], F32)
-        make_identity(nc, identity[:])
-        identity_bf = keep.tile([P, P], BF16)
-        make_identity(nc, identity_bf[:])
-
-        x_bf = keep.tile([P, BATCHES], BF16)
-        with nc.allow_non_contiguous_dma(reason="512 scalars, one token to a partition"):
-            nc.sync.dma_start(out=x_bf[:], in_=input_numeric.rearrange("b s o -> s (b o)"))
-        x_col = keep.tile([P, BATCHES], F32)
-        nc.vector.tensor_copy(out=x_col[:], in_=x_bf[:])
-
-        w_all = keep.tile([P, VECTOR_CHUNKS * CHUNK], BF16)
-        b_all = keep.tile([P, VECTOR_CHUNKS * CHUNK], BF16)
         proj_loaded = keep.tile([P, 2, P], BF16)
         nc.sync.dma_start(out=proj_loaded[:, 0, :], in_=proj_w.rearrange("(a p) o -> a (p o)", p=P))
         nc.sync.dma_start(out=proj_loaded[:, 1, :], in_=proj_b.rearrange("(a p) -> a p", p=P))
-        proj_turned = psum_out.tile([P, 2, P], BF16, tag="row_acc")
-        nc.tensor.transpose(proj_turned[:, 0, :], proj_loaded[:, 0, :], identity_bf[:])
-        nc.tensor.transpose(proj_turned[:, 1, :], proj_loaded[:, 1, :], identity_bf[:])
-        proj_cols = keep.tile([P, 2, P], BF16)
-        nc.vector.tensor_copy(out=proj_cols[:], in_=proj_turned[:])
+        x_bf = keep.tile([P, BATCHES], BF16)
+        with nc.allow_non_contiguous_dma(reason="512 scalars, one token to a partition"):
+            nc.sync.dma_start(out=x_bf[:], in_=input_numeric.rearrange("b s o -> s (b o)"))
+
+        identity_bf = keep.tile([P, P], BF16)
+        make_identity(nc, identity_bf[:])
+        identity = keep.tile([P, P], F32)
+        make_identity(nc, identity[:])
+
+        head_bank = psum_out.tile([P, 2, P], BF16, tag="row_acc")
+        nc.tensor.transpose(head_bank[:, 0, :], proj_loaded[:, 0, :], identity_bf[:])
+        nc.tensor.transpose(head_bank[:, 1, :], proj_loaded[:, 1, :], identity_bf[:])
+        proj_cols = keep.tile([P, 2, P], F32)
+        nc.vector.tensor_copy(out=proj_cols[:], in_=head_bank[:])
+        x_bank = psum_turn.tile([P, BATCHES, P], BF16, tag="turn_bank")
+        for b in range(BATCHES):
+            nc.tensor.transpose(x_bank[:, b, :], x_bf[:, b : b + 1].to_broadcast([P, P]), identity_bf[:])
+        x_rows = keep.tile([P, BATCHES, P], F32)
+        nc.vector.tensor_copy(out=x_rows[:], in_=x_bank[:])
 
         x_pair = keep.tile([P, BATCHES, P], BF16)
-        nc.vector.memset(x_pair[:], 0.0)
-        nc.vector.memset(x_pair[ONES_PARTITION : ONES_PARTITION + 1, :, :], 1.0)
+        nc.gpsimd.memset(x_pair[:], 0.0)
+        nc.gpsimd.memset(x_pair[ONES_PARTITION : ONES_PARTITION + 1, :, :], 1.0)
         nc.sync.dma_start(out=x_pair[0:1, :, :], in_=input_numeric.rearrange("b s o -> o b s"))
-        proj_pair = keep.tile([P, TENSOR_CHUNKS, CHUNK], BF16)
-        nc.vector.memset(proj_pair[:], 0.0)
-        for i in range(TENSOR_CHUNKS):
-            cols = slice(i * TENSOR_EVERY * CHUNK, (i * TENSOR_EVERY + 1) * CHUNK)
-            nc.sync.dma_start(out=proj_pair[0:1, i, :], in_=proj_w[cols, :].rearrange("n o -> o n"))
+        proj_pair = keep.tile([P, TENSOR_SHARE, SLICES // TENSOR_OF, SLICE], BF16)
+        nc.gpsimd.memset(proj_pair[:], 0.0)
+        w_view = proj_w.rearrange("(q i n) o -> o i q n", i=TENSOR_OF, n=SLICE)
+        b_view = proj_b.rearrange("(o q i n) -> o i q n", o=1, i=TENSOR_OF, n=SLICE)
+        for slot, residue in enumerate(TENSOR_RESIDUES):
+            nc.sync.dma_start(out=proj_pair[0:1, slot, :, :], in_=w_view[:, residue, :, :])
             nc.sync.dma_start(
-                out=proj_pair[ONES_PARTITION : ONES_PARTITION + 1, i, :], in_=proj_b[cols].unsqueeze(0)
+                out=proj_pair[ONES_PARTITION : ONES_PARTITION + 1, slot, :, :], in_=b_view[:, residue, :, :]
             )
-
-        def vector_slot(j):
-            return j - j // TENSOR_EVERY - 1
 
         table_codes = keep.tile([P, PASSES, DIM], U32, align_bytes=64)
         table_scales = keep.tile([P, PASSES // PLANES, DIM], U8, align_bytes=64)
 
         def table_plane(g):
             return table_scales[PLANE_ROWS * (g % PLANES) : P, g // PLANES, :]
-
-        spread_banks = {}
-
-        def spread_projection(j, which):
-            for half in range(SPREAD_BANKS):
-                spread_bank = psum_turn.tile([P, BANK_TILES, P], BF16, tag="turn_bank")
-                for i in range(BANK_TILES):
-                    a = (SPREAD_BANKS * j + half) * BANK_TILES + i
-                    nc.tensor.transpose(
-                        spread_bank[:, i, :],
-                        proj_cols[:, which, a : a + 1].to_broadcast([P, P]),
-                        identity_bf[:],
-                    )
-                spread_banks[(j, which, half)] = spread_bank
-
-        def collect_projection(j, which):
-            target = b_all if which else w_all
-            for half in range(SPREAD_BANKS):
-                first = (SPREAD_BANKS * vector_slot(j) + half) * BANK_TILES * P
-                nc.scalar.copy(
-                    out=target[:, first : first + BANK_TILES * P],
-                    in_=spread_banks[(j, which, half)][:].rearrange("p i n -> p (i n)"),
-                )
 
         table_rows = {}
         table_grouped = {}
@@ -155,106 +132,77 @@ def tile_softembedding_k_kernel(tc, input_numeric, proj_w, proj_b, emb_table, ou
         neg_max = {}
         part_sum = {}
         neg_top = {}
-        chunk_scale = {}
+        slice_scale = {}
 
-        def logits(k):
-            b, j = divmod(k, CHUNKS)
-            if j == 0:
-                row_neg_max = stats.tile([P, CHUNKS], F32)
-                row_part_sum = stats.tile([P, CHUNKS, CHUNK_BANKS], F32)
-                nc.vector.memset(row_part_sum[:], 0.0)
+        def logits(q):
+            b, i = divmod(q, SLICES)
+            if i == 0:
+                row_neg_max = stats.tile([P, SLICES], F32)
+                row_part_sum = stats.tile([P, SLICES], F32)
                 neg_max[b] = row_neg_max
                 part_sum[b] = row_part_sum
-            chunk = exp_pool.tile([P, CHUNK], F32)
-            exps[k] = chunk
-            if j % TENSOR_EVERY == 0:
-                logit_banks[k] = []
-                for bank_no in range(CHUNK_BANKS):
-                    logit_bank = psum_logit.tile([P, BANK], F32)
-                    nc.tensor.matmul(
-                        out=logit_bank[:],
-                        lhsT=x_pair[:, b, :],
-                        rhs=proj_pair[:, j // TENSOR_EVERY, bank_no * BANK : (bank_no + 1) * BANK],
-                        start=True,
-                        stop=True,
-                    )
-                    logit_banks[k].append(logit_bank)
-            else:
-                cols = slice(vector_slot(j) * CHUNK, (vector_slot(j) + 1) * CHUNK)
-                nc.vector.scalar_tensor_tensor(
-                    out=chunk[:],
-                    in0=w_all[:, cols],
-                    scalar=x_col[:, b : b + 1],
-                    in1=b_all[:, cols],
-                    op0=ALU.mult,
-                    op1=ALU.add,
-                )
-
-        def maximum(k):
-            b, j = divmod(k, CHUNKS)
-            if j % TENSOR_EVERY == 0:
-                bank_neg_max = stats.tile([P, CHUNK_BANKS], F32)
-                for bank_no in range(CHUNK_BANKS):
-                    nc.vector.tensor_reduce(
-                        out=bank_neg_max[:, bank_no : bank_no + 1],
-                        in_=logit_banks[k][bank_no][:],
-                        axis=AXIS.X,
-                        op=ALU.max,
-                        negate=True,
-                    )
-                nc.vector.tensor_reduce(
-                    out=neg_max[b][:, j : j + 1], in_=bank_neg_max[:], axis=AXIS.X, op=ALU.min
+            logit_bank = psum_logit.tile([P, SLICE], F32)
+            if i % TENSOR_OF in TENSOR_RESIDUES:
+                nc.tensor.matmul(
+                    out=logit_bank[:],
+                    lhsT=x_pair[:, b, :],
+                    rhs=proj_pair[:, TENSOR_RESIDUES.index(i % TENSOR_OF), i // TENSOR_OF, :],
+                    start=True,
+                    stop=True,
                 )
             else:
-                nc.vector.tensor_reduce(
-                    out=neg_max[b][:, j : j + 1], in_=exps[k][:], axis=AXIS.X, op=ALU.max, negate=True
-                )
-
-        def exponentials(k):
-            b, j = divmod(k, CHUNKS)
-            if j % TENSOR_EVERY == 0:
-                for bank_no in range(CHUNK_BANKS):
-                    nc.scalar.activation(
-                        out=exps[k][:, bank_no * BANK : (bank_no + 1) * BANK],
-                        in_=logit_banks[k][bank_no][:],
-                        func=ACT.Exp,
-                        bias=neg_max[b][:, j : j + 1],
-                        scale=1.0,
-                        accum_out=part_sum[b][:, j, bank_no : bank_no + 1],
+                slice_cols = logit_cols.tile([P, COLS, P], F32)
+                for c in range(COLS):
+                    a = COLS * i + c
+                    nc.vector.tensor_scalar(
+                        out=slice_cols[:, c, :],
+                        in0=x_rows[:, b, :],
+                        scalar1=proj_cols[:, 0, a : a + 1],
+                        scalar2=proj_cols[:, 1, a : a + 1],
+                        op0=ALU.mult,
+                        op1=ALU.add,
                     )
-            else:
-                nc.scalar.activation(
-                    out=exps[k][:],
-                    in_=exps[k][:],
-                    func=ACT.Exp,
-                    bias=neg_max[b][:, j : j + 1],
-                    scale=1.0,
-                    accum_out=part_sum[b][:, j, 0:1],
-                )
+                for c in range(COLS):
+                    nc.tensor.transpose(logit_bank[:, c * P : (c + 1) * P], slice_cols[:, c, :], identity[:])
+            logit_banks[q] = logit_bank
 
-        def row_top(b):
-            top = stats.tile([P, 1], F32)
-            nc.vector.tensor_reduce(out=top[:], in_=neg_max[b][:], axis=AXIS.X, op=ALU.min)
-            neg_top[b] = top
+        def maximum(q):
+            b, i = divmod(q, SLICES)
+            nc.vector.tensor_reduce(
+                out=neg_max[b][:, i : i + 1], in_=logit_banks[q][:], axis=AXIS.X, op=ALU.max, negate=True
+            )
+
+        def exponentials(q):
+            b, i = divmod(q, SLICES)
+            if i % CHUNK_SLICES == 0:
+                chunk_exps = exp_pool.tile([P, CHUNK], F32)
+                exps[q // CHUNK_SLICES] = chunk_exps
+            first = i % CHUNK_SLICES * SLICE
+            nc.scalar.activation(
+                out=exps[q // CHUNK_SLICES][:, first : first + SLICE],
+                in_=logit_banks[q][:],
+                func=ACT.Exp,
+                bias=neg_max[b][:, i : i + 1],
+                scale=1.0,
+                accum_out=part_sum[b][:, i : i + 1],
+            )
 
         def row_scales(b):
-            factor = stats.tile([P, CHUNKS], F32)
-            nc.scalar.activation(
-                out=factor[:], in_=neg_max[b][:], func=ACT.Exp, bias=neg_top[b][:, 0:1], scale=-1.0
-            )
-            chunk_sum = stats.tile([P, CHUNKS], F32)
-            nc.vector.tensor_reduce(out=chunk_sum[:], in_=part_sum[b][:], axis=AXIS.X, op=ALU.add)
-            weighted = stats.tile([P, CHUNKS], F32)
-            nc.vector.tensor_tensor(out=weighted[:], in0=factor[:], in1=chunk_sum[:], op=ALU.mult)
+            top = stats.tile([P, 1], F32)
+            nc.vector.tensor_reduce(out=top[:], in_=neg_max[b][:], axis=AXIS.X, op=ALU.min)
+            factor = stats.tile([P, SLICES], F32)
+            nc.scalar.activation(out=factor[:], in_=neg_max[b][:], func=ACT.Exp, bias=top[:, 0:1], scale=-1.0)
+            weighted = stats.tile([P, SLICES], F32)
+            nc.vector.tensor_tensor(out=weighted[:], in0=factor[:], in1=part_sum[b][:], op=ALU.mult)
             total = stats.tile([P, 1], F32)
             nc.vector.tensor_reduce(out=total[:], in_=weighted[:], axis=AXIS.X, op=ALU.add)
             inv_total = stats.tile([P, 1], F32)
             nc.vector.reciprocal(out=inv_total[:], in_=total[:])
-            row_chunk_scale = stats.tile([P, CHUNKS], F32)
+            row_slice_scale = stats.tile([P, SLICES], F32)
             nc.vector.tensor_scalar(
-                out=row_chunk_scale[:], in0=factor[:], scalar1=inv_total[:, 0:1], scalar2=None, op0=ALU.mult
+                out=row_slice_scale[:], in0=factor[:], scalar1=inv_total[:, 0:1], scalar2=None, op0=ALU.mult
             )
-            chunk_scale[b] = row_chunk_scale
+            slice_scale[b] = row_slice_scale
 
         weights = {}
         turned = {}
@@ -263,21 +211,21 @@ def tile_softembedding_k_kernel(tc, input_numeric, proj_w, proj_b, emb_table, ou
         weight_scales = {}
         acc = {}
 
-        def normalise(stage, k, on_scalar):
+        def normalise(stage, k, scalar_slices):
             b, j = divmod(k, CHUNKS)
             chunk_weights = stage.tile([P, CHUNK], BF16)
-            if on_scalar:
-                nc.scalar.activation(
-                    out=chunk_weights[:], in_=exps[k][:], func=ACT.Copy, scale=chunk_scale[b][:, j : j + 1]
-                )
-            else:
-                nc.vector.tensor_scalar(
-                    out=chunk_weights[:],
-                    in0=exps[k][:],
-                    scalar1=chunk_scale[b][:, j : j + 1],
-                    scalar2=None,
-                    op0=ALU.mult,
-                )
+            for c in range(CHUNK_SLICES):
+                cols = slice(c * SLICE, (c + 1) * SLICE)
+                i = j * CHUNK_SLICES + c
+                scale = slice_scale[b][:, i : i + 1]
+                if c in scalar_slices:
+                    nc.scalar.activation(
+                        out=chunk_weights[:, cols], in_=exps[k][:, cols], func=ACT.Copy, scale=scale
+                    )
+                else:
+                    nc.vector.tensor_scalar(
+                        out=chunk_weights[:, cols], in0=exps[k][:, cols], scalar1=scale, scalar2=None, op0=ALU.mult
+                    )
             weights[k] = chunk_weights
 
         def turn(k):
@@ -337,55 +285,42 @@ def tile_softembedding_k_kernel(tc, input_numeric, proj_w, proj_b, emb_table, ou
             nc.scalar.copy(out=result[:], in_=acc[b][:])
             nc.sync.dma_start(out=out[b], in_=result[:])
 
+        def softmax_step(q):
+            if q < TOTAL_SLICES:
+                logits(q)
+            if 0 <= q - 1 < TOTAL_SLICES:
+                maximum(q - 1)
+            if 0 <= q - EXP_LAG < TOTAL_SLICES:
+                exponentials(q - EXP_LAG)
+                if (q - EXP_LAG) % SLICES == SLICES - 1:
+                    row_scales((q - EXP_LAG) // SLICES)
 
         with tc.tile_pool(name="table_stage", bufs=1) as table_stage:
             for g in range(TABLE_AHEAD):
                 load_table(table_stage, g)
-            for k in range(CHUNKS):
-                spread_next = k + 1 < CHUNKS and (k + 1) % TENSOR_EVERY != 0
-                for quarter in range(CHUNK_PASSES):
-                    g = k * CHUNK_PASSES + quarter
-                    if g + TABLE_AHEAD < PASSES:
-                        load_table(table_stage, g + TABLE_AHEAD)
-                    regroup_table(table_stage, g)
-                    if g >= TABLE_LAG:
-                        quantise_table(g - TABLE_LAG)
-                    if quarter == 0:
-                        logits(k)
-                        if k >= 1:
-                            exponentials(k - 1)
-                    if quarter == 1:
-                        maximum(k)
-                    if quarter < 2 and spread_next:
-                        spread_projection(k + 1, quarter)
-                    if quarter >= 2 and spread_next:
-                        collect_projection(k + 1, quarter - 2)
+            for q in range(PASSES):
+                if q + TABLE_AHEAD < PASSES:
+                    load_table(table_stage, q + TABLE_AHEAD)
+                regroup_table(table_stage, q)
+                if q >= TABLE_LAG:
+                    quantise_table(q - TABLE_LAG)
+                softmax_step(q)
             for g in range(PASSES - TABLE_LAG, PASSES):
                 quantise_table(g)
 
         with tc.tile_pool(name="weight_stage", bufs=2, reuse_waits="tile") as weight_stage:
-            for k in range(CHUNKS, TOTAL + MULTIPLY_LAG):
-                row_ends = k % CHUNKS == 0 and k <= TOTAL
-                if row_ends:
-                    row_top(k // CHUNKS - 1)
-                if k < TOTAL:
-                    logits(k)
-                    maximum(k)
-                on_scalar = k < TOTAL and k % 2 == 1
-                if k - NORMALISE_LAG < TOTAL and on_scalar:
-                    normalise(weight_stage, k - NORMALISE_LAG, True)
-                    turn(k - NORMALISE_LAG)
-                if k - 1 < TOTAL:
-                    exponentials(k - 1)
-                if row_ends:
-                    row_scales(k // CHUNKS - 1)
-                if k - NORMALISE_LAG < TOTAL and not on_scalar:
-                    normalise(weight_stage, k - NORMALISE_LAG, False)
-                    turn(k - NORMALISE_LAG)
-                if 0 <= k - REGROUP_LAG < TOTAL:
-                    regroup(weight_stage, k - REGROUP_LAG)
-                if 0 <= k - MULTIPLY_LAG:
-                    quantise(weight_stage, k - MULTIPLY_LAG)
-                    multiply(k - MULTIPLY_LAG)
-                    if (k - MULTIPLY_LAG) % CHUNKS == CHUNKS - 1:
-                        store(weight_stage, (k - MULTIPLY_LAG) // CHUNKS)
+            for q in range(SLICES, SLICES * (BATCHES + 1) + NORMALISE_LAG):
+                softmax_step(q)
+                k, rest = divmod(q - NORMALISE_LAG, CHUNK_SLICES)
+                if rest != 0:
+                    continue
+                if 0 <= k < TOTAL_CHUNKS:
+                    normalise(weight_stage, k, (1,))
+                    turn(k)
+                if 0 <= k - 1 < TOTAL_CHUNKS:
+                    regroup(weight_stage, k - 1)
+                if 0 <= k - 2 < TOTAL_CHUNKS:
+                    quantise(weight_stage, k - 2)
+                    multiply(k - 2)
+                    if (k - 2) % CHUNKS == CHUNKS - 1:
+                        store(weight_stage, (k - 2) // CHUNKS)

@@ -19,28 +19,28 @@ DIM = 512
 PACK = 4
 K_PASS = P * PACK
 PASSES = VOCAB // K_PASS
-SLICE = 512
-SLICES = VOCAB // SLICE
-TOTAL_SLICES = BATCHES * SLICES
-COLS = SLICE // P
-CHUNK = 2048
-CHUNKS = VOCAB // CHUNK
-CHUNK_PASSES = CHUNK // K_PASS
-CHUNK_SLICES = CHUNK // SLICE
-TOTAL_CHUNKS = BATCHES * CHUNKS
-BANK_PASSES = 2
+TOTAL = BATCHES * PASSES
+COLS = K_PASS // P
+PAIR = 2
 PLANES = 4
 PLANE_ROWS = 4
 RUN = 4
+VECTOR_COLS = 240
 TENSOR_SHARE = 3
 TENSOR_OF = 8
 TENSOR_RESIDUES = [i for i in range(TENSOR_OF) if TENSOR_SHARE * i % TENSOR_OF < TENSOR_SHARE]
 ONES_PARTITION = 32
-EXP_BUFS = CHUNKS + 2
-TABLE_AHEAD = 2
-TABLE_LAG = 2
+TABLE_AHEAD = 3
+TABLE_LAG = 1
+MAX_LAG = 1
 EXP_LAG = 2
-NORMALISE_LAG = SLICES + EXP_LAG
+TOP_LAG = 2
+FACTOR_LAG = 3
+TOTAL_LAG = 4
+INVERSE_LAG = 5
+SCALE_LAG = 6
+NORMALISE_LAG = PASSES + SCALE_LAG
+EXP_BUFS = NORMALISE_LAG - EXP_LAG + 3
 
 FLOPS = 2 * BATCHES * P * VOCAB * DIM
 
@@ -52,6 +52,8 @@ def tile_softembedding_k_kernel(tc, input_numeric, proj_w, proj_b, emb_table, ou
         exp_pool = ctx.enter_context(tc.tile_pool(name="exp_pool", bufs=EXP_BUFS))
         logit_cols = ctx.enter_context(tc.tile_pool(name="logit_cols", bufs=3))
         stats = ctx.enter_context(tc.tile_pool(name="stats", bufs=2))
+        table_stage = ctx.enter_context(tc.tile_pool(name="table_stage", bufs=4))
+        weight_stage = ctx.enter_context(tc.tile_pool(name="weight_stage", bufs=3))
         psum_logit = ctx.enter_context(tc.psum_pool(name="psum_logit", bufs=4))
         psum_turn = ctx.enter_context(tc.psum_pool(name="psum_turn", bufs=3))
         psum_out = ctx.enter_context(tc.psum_pool(name="psum_out", bufs=1))
@@ -83,10 +85,10 @@ def tile_softembedding_k_kernel(tc, input_numeric, proj_w, proj_b, emb_table, ou
         nc.gpsimd.memset(x_pair[:], 0.0)
         nc.gpsimd.memset(x_pair[ONES_PARTITION : ONES_PARTITION + 1, :, :], 1.0)
         nc.sync.dma_start(out=x_pair[0:1, :, :], in_=input_numeric.rearrange("b s o -> o b s"))
-        proj_pair = keep.tile([P, TENSOR_SHARE, SLICES // TENSOR_OF, SLICE], BF16)
+        proj_pair = keep.tile([P, TENSOR_SHARE, PASSES // TENSOR_OF, K_PASS], BF16)
         nc.gpsimd.memset(proj_pair[:], 0.0)
-        w_view = proj_w.rearrange("(q i n) o -> o i q n", i=TENSOR_OF, n=SLICE)
-        b_view = proj_b.rearrange("(o q i n) -> o i q n", o=1, i=TENSOR_OF, n=SLICE)
+        w_view = proj_w.rearrange("(q i n) o -> o i q n", i=TENSOR_OF, n=K_PASS)
+        b_view = proj_b.rearrange("(o q i n) -> o i q n", o=1, i=TENSOR_OF, n=K_PASS)
         for slot, residue in enumerate(TENSOR_RESIDUES):
             nc.sync.dma_start(out=proj_pair[0:1, slot, :, :], in_=w_view[:, residue, :, :])
             nc.sync.dma_start(
@@ -102,22 +104,21 @@ def tile_softembedding_k_kernel(tc, input_numeric, proj_w, proj_b, emb_table, ou
         table_rows = {}
         table_grouped = {}
 
-        def load_table(stage, g):
-            pass_rows = stage.tile([P, PACK, DIM], BF16, bufs=TABLE_AHEAD + 1)
+        def load_table(g):
+            pass_rows = table_stage.tile([P, PACK, DIM], BF16)
             nc.sync.dma_start(
                 out=pass_rows[:],
                 in_=emb_table[g * K_PASS : (g + 1) * K_PASS, :].rearrange("(p t) d -> p t d", t=PACK),
             )
             table_rows[g] = pass_rows
 
-        def regroup_table(stage, g):
-            pass_grouped = stage.tile([P, DIM, PACK], BF16, align_bytes=64, bufs=TABLE_LAG + 2)
+        def regroup_table(g):
+            pass_grouped = table_stage.tile([P, DIM, PACK], BF16, align_bytes=64)
             dst = pass_grouped[:].rearrange("p (r i) t -> p r t i", i=RUN)
             src = table_rows[g][:].rearrange("p t (r i) -> p r t i", i=RUN)
-            if g % 2 == 0:
-                nc.vector.tensor_copy(out=dst, in_=src)
-            else:
-                nc.scalar.copy(out=dst, in_=src)
+            cut = VECTOR_COLS // RUN
+            nc.vector.tensor_copy(out=dst[:, :cut, :, :], in_=src[:, :cut, :, :])
+            nc.scalar.copy(out=dst[:, cut:, :, :], in_=src[:, cut:, :, :])
             table_grouped[g] = pass_grouped
 
         def quantise_table(g):
@@ -127,22 +128,45 @@ def tile_softembedding_k_kernel(tc, input_numeric, proj_w, proj_b, emb_table, ou
                 in_=table_grouped[g][:].rearrange("p d t -> p (d t)"),
             )
 
-        exps = {}
+        slice_cols = {}
         logit_banks = {}
+        exps = {}
         neg_max = {}
         part_sum = {}
         neg_top = {}
+        factors = {}
+        inverse = {}
         slice_scale = {}
 
-        def logits(q):
-            b, i = divmod(q, SLICES)
+        def by_tensor(q):
+            return q % TENSOR_OF in TENSOR_RESIDUES
+
+        def columns(q):
+            b, i = divmod(q, PASSES)
             if i == 0:
-                row_neg_max = stats.tile([P, SLICES], F32)
-                row_part_sum = stats.tile([P, SLICES], F32)
+                row_neg_max = stats.tile([P, PASSES], F32)
+                row_part_sum = stats.tile([P, PASSES], F32)
                 neg_max[b] = row_neg_max
                 part_sum[b] = row_part_sum
-            logit_bank = psum_logit.tile([P, SLICE], F32)
-            if i % TENSOR_OF in TENSOR_RESIDUES:
+            if by_tensor(q):
+                return
+            cols = logit_cols.tile([P, COLS, P], F32)
+            for c in range(COLS):
+                a = COLS * i + c
+                nc.vector.tensor_scalar(
+                    out=cols[:, c, :],
+                    in0=x_rows[:, b, :],
+                    scalar1=proj_cols[:, 0, a : a + 1],
+                    scalar2=proj_cols[:, 1, a : a + 1],
+                    op0=ALU.mult,
+                    op1=ALU.add,
+                )
+            slice_cols[q] = cols
+
+        def logits(q):
+            b, i = divmod(q, PASSES)
+            logit_bank = psum_logit.tile([P, K_PASS], F32)
+            if by_tensor(q):
                 nc.tensor.matmul(
                     out=logit_bank[:],
                     lhsT=x_pair[:, b, :],
@@ -151,56 +175,57 @@ def tile_softembedding_k_kernel(tc, input_numeric, proj_w, proj_b, emb_table, ou
                     stop=True,
                 )
             else:
-                slice_cols = logit_cols.tile([P, COLS, P], F32)
                 for c in range(COLS):
-                    a = COLS * i + c
-                    nc.vector.tensor_scalar(
-                        out=slice_cols[:, c, :],
-                        in0=x_rows[:, b, :],
-                        scalar1=proj_cols[:, 0, a : a + 1],
-                        scalar2=proj_cols[:, 1, a : a + 1],
-                        op0=ALU.mult,
-                        op1=ALU.add,
-                    )
-                for c in range(COLS):
-                    nc.tensor.transpose(logit_bank[:, c * P : (c + 1) * P], slice_cols[:, c, :], identity[:])
+                    nc.tensor.transpose(logit_bank[:, c * P : (c + 1) * P], slice_cols[q][:, c, :], identity[:])
             logit_banks[q] = logit_bank
 
         def maximum(q):
-            b, i = divmod(q, SLICES)
+            b, i = divmod(q, PASSES)
             nc.vector.tensor_reduce(
                 out=neg_max[b][:, i : i + 1], in_=logit_banks[q][:], axis=AXIS.X, op=ALU.max, negate=True
             )
 
         def exponentials(q):
-            b, i = divmod(q, SLICES)
-            if i % CHUNK_SLICES == 0:
-                chunk_exps = exp_pool.tile([P, CHUNK], F32)
-                exps[q // CHUNK_SLICES] = chunk_exps
-            first = i % CHUNK_SLICES * SLICE
+            b, i = divmod(q, PASSES)
+            slice_exps = exp_pool.tile([P, K_PASS], F32)
             nc.scalar.activation(
-                out=exps[q // CHUNK_SLICES][:, first : first + SLICE],
+                out=slice_exps[:],
                 in_=logit_banks[q][:],
                 func=ACT.Exp,
                 bias=neg_max[b][:, i : i + 1],
                 scale=1.0,
                 accum_out=part_sum[b][:, i : i + 1],
             )
+            exps[q] = slice_exps
 
-        def row_scales(b):
+        def row_top(b):
             top = stats.tile([P, 1], F32)
             nc.vector.tensor_reduce(out=top[:], in_=neg_max[b][:], axis=AXIS.X, op=ALU.min)
-            factor = stats.tile([P, SLICES], F32)
-            nc.scalar.activation(out=factor[:], in_=neg_max[b][:], func=ACT.Exp, bias=top[:, 0:1], scale=-1.0)
-            weighted = stats.tile([P, SLICES], F32)
-            nc.vector.tensor_tensor(out=weighted[:], in0=factor[:], in1=part_sum[b][:], op=ALU.mult)
+            neg_top[b] = top
+
+        def row_factors(b):
+            factor = stats.tile([P, PASSES], F32)
+            nc.scalar.activation(
+                out=factor[:], in_=neg_max[b][:], func=ACT.Exp, bias=neg_top[b][:, 0:1], scale=-1.0
+            )
+            factors[b] = factor
+
+        def row_total(b):
+            weighted = stats.tile([P, PASSES], F32)
+            nc.vector.tensor_tensor(out=weighted[:], in0=factors[b][:], in1=part_sum[b][:], op=ALU.mult)
             total = stats.tile([P, 1], F32)
             nc.vector.tensor_reduce(out=total[:], in_=weighted[:], axis=AXIS.X, op=ALU.add)
+            inverse[b] = total
+
+        def row_inverse(b):
             inv_total = stats.tile([P, 1], F32)
-            nc.vector.reciprocal(out=inv_total[:], in_=total[:])
-            row_slice_scale = stats.tile([P, SLICES], F32)
+            nc.vector.reciprocal(out=inv_total[:], in_=inverse[b][:])
+            inverse[b] = inv_total
+
+        def row_scales(b):
+            row_slice_scale = stats.tile([P, PASSES], F32)
             nc.vector.tensor_scalar(
-                out=row_slice_scale[:], in0=factor[:], scalar1=inv_total[:, 0:1], scalar2=None, op0=ALU.mult
+                out=row_slice_scale[:], in0=factors[b][:], scalar1=inverse[b][:, 0:1], scalar2=None, op0=ALU.mult
             )
             slice_scale[b] = row_slice_scale
 
@@ -211,116 +236,119 @@ def tile_softembedding_k_kernel(tc, input_numeric, proj_w, proj_b, emb_table, ou
         weight_scales = {}
         acc = {}
 
-        def normalise(stage, k, scalar_slices):
-            b, j = divmod(k, CHUNKS)
-            chunk_weights = stage.tile([P, CHUNK], BF16)
-            for c in range(CHUNK_SLICES):
-                cols = slice(c * SLICE, (c + 1) * SLICE)
-                i = j * CHUNK_SLICES + c
-                scale = slice_scale[b][:, i : i + 1]
-                if c in scalar_slices:
-                    nc.scalar.activation(
-                        out=chunk_weights[:, cols], in_=exps[k][:, cols], func=ACT.Copy, scale=scale
-                    )
-                else:
-                    nc.vector.tensor_scalar(
-                        out=chunk_weights[:, cols], in0=exps[k][:, cols], scalar1=scale, scalar2=None, op0=ALU.mult
-                    )
-            weights[k] = chunk_weights
+        def normalise(m, on_scalar):
+            b, i = divmod(m, PASSES)
+            pair, c = divmod(m, PAIR)
+            if c == 0:
+                pair_weights = weight_stage.tile([P, PAIR, 2, P, 2], BF16)
+                weights[pair] = pair_weights
+            target = weights[pair][:, c, :, :, :]
+            source = exps[m][:].rearrange("s (p u e) -> s u p e", u=2, e=2)
+            scale = slice_scale[b][:, i : i + 1]
+            if on_scalar:
+                nc.scalar.activation(out=target, in_=source, func=ACT.Copy, scale=scale)
+            else:
+                nc.vector.tensor_scalar(out=target, in0=source, scalar1=scale, scalar2=None, op0=ALU.mult)
 
-        def turn(k):
-            words = weights[k][:].bitcast(F32)
-            turned[k] = []
-            for half in range(CHUNK_PASSES // BANK_PASSES):
-                turned_bank = psum_turn.tile([P, BANK_PASSES, 2, P], F32, tag="turn_bank")
-                for c in range(BANK_PASSES):
-                    for u in range(2):
-                        first = (BANK_PASSES * half + c) * 2 * P
-                        nc.tensor.transpose(
-                            turned_bank[:, c, u, :], words[:, first + u : first + 2 * P : 2], identity[:]
-                        )
-                turned[k].append(turned_bank)
+        def turn(pair):
+            words = weights[pair][:].rearrange("s c u p e -> s (c u p e)").bitcast(F32)
+            turned_bank = psum_turn.tile([P, PAIR, 2, P], F32, tag="turn_bank")
+            for c in range(PAIR):
+                for u in range(2):
+                    first = (2 * c + u) * P
+                    nc.tensor.transpose(turned_bank[:, c, u, :], words[:, first : first + P], identity[:])
+            turned[pair] = turned_bank
 
-        def regroup(stage, k):
-            chunk_grouped = stage.tile([P, CHUNK_PASSES, P, PACK], BF16, align_bytes=64)
-            grouped_words = chunk_grouped[:].bitcast(F32)
-            for half in range(CHUNK_PASSES // BANK_PASSES):
-                nc.scalar.copy(
-                    out=grouped_words[:, BANK_PASSES * half : BANK_PASSES * (half + 1), :, :],
-                    in_=turned[k][half][:].rearrange("p c u s -> p c s u"),
-                )
-            weight_grouped[k] = chunk_grouped
+        def regroup(pair):
+            pair_grouped = weight_stage.tile([P, PAIR, P, PACK], BF16, align_bytes=64)
+            nc.scalar.copy(out=pair_grouped[:].bitcast(F32), in_=turned[pair][:].rearrange("p c u s -> p c s u"))
+            weight_grouped[pair] = pair_grouped
 
-        def quantise(stage, k):
-            chunk_codes = stage.tile([P, CHUNK_PASSES * P], U32, align_bytes=64)
-            chunk_planes = stage.tile([P, CHUNK_PASSES * P], U8, align_bytes=64)
+        def quantise(pair):
+            pair_codes = weight_stage.tile([P, PAIR * P], U32, align_bytes=64)
+            pair_planes = weight_stage.tile([P, PAIR * P], U8, align_bytes=64)
             nc.vector.quantize_mx(
-                out=chunk_codes[:].bitcast(FP8X4),
-                scales=chunk_planes[:],
-                in_=weight_grouped[k][:].rearrange("p c s t -> p (c s t)"),
+                out=pair_codes[:].bitcast(FP8X4),
+                scales=pair_planes[:],
+                in_=weight_grouped[pair][:].rearrange("p c s t -> p (c s t)"),
             )
-            weight_codes[k] = chunk_codes
-            weight_scales[k] = chunk_planes
+            weight_codes[pair] = pair_codes
+            weight_scales[pair] = pair_planes
 
-        def multiply(k):
-            b, j = divmod(k, CHUNKS)
-            if j == 0:
+        def multiply(pair):
+            b, row_pair = divmod(pair, PASSES // PAIR)
+            if row_pair == 0:
                 row_acc = psum_out.tile([P, DIM], F32)
                 acc[b] = row_acc
-            for c in range(CHUNK_PASSES):
-                g = j * CHUNK_PASSES + c
+            for c in range(PAIR):
+                g = row_pair * PAIR + c
                 tokens = slice(c * P, (c + 1) * P)
                 nc.tensor.matmul_mx(
                     out=acc[b][:],
-                    lhsT=weight_codes[k][:, tokens].bitcast(FP8X4),
-                    lhsT_scale=weight_scales[k][:, tokens],
+                    lhsT=weight_codes[pair][:, tokens].bitcast(FP8X4),
+                    lhsT_scale=weight_scales[pair][:, tokens],
                     rhs=table_codes[:, g, :].bitcast(FP8X4),
                     rhs_scale=table_plane(g),
                     start=(g == 0),
                     stop=(g == PASSES - 1),
                 )
 
-        def store(stage, b):
-            result = stage.tile([P, DIM], F32)
+        def store(b):
+            result = weight_stage.tile([P, DIM], F32)
             nc.scalar.copy(out=result[:], in_=acc[b][:])
             nc.sync.dma_start(out=out[b], in_=result[:])
 
+        def row_of_last(q):
+            return q // PASSES if 0 <= q < TOTAL and q % PASSES == PASSES - 1 else None
+
         def softmax_step(q):
-            if q < TOTAL_SLICES:
+            if q + 1 < TOTAL:
+                columns(q + 1)
+            if q < TOTAL:
                 logits(q)
-            if 0 <= q - 1 < TOTAL_SLICES:
-                maximum(q - 1)
-            if 0 <= q - EXP_LAG < TOTAL_SLICES:
+            if 0 <= q - MAX_LAG < TOTAL:
+                maximum(q - MAX_LAG)
+            if 0 <= q - EXP_LAG < TOTAL:
                 exponentials(q - EXP_LAG)
-                if (q - EXP_LAG) % SLICES == SLICES - 1:
-                    row_scales((q - EXP_LAG) // SLICES)
+            for lag, stage in (
+                (TOP_LAG, row_top),
+                (FACTOR_LAG, row_factors),
+                (TOTAL_LAG, row_total),
+                (INVERSE_LAG, row_inverse),
+                (SCALE_LAG, row_scales),
+            ):
+                b = row_of_last(q - lag)
+                if b is not None:
+                    stage(b)
 
-        with tc.tile_pool(name="table_stage", bufs=1) as table_stage:
+        def weight_step(m, scalar_share):
+            pair, c = divmod(m, PAIR)
+            if 0 <= m < TOTAL:
+                normalise(m, m % 4 in scalar_share)
+            last_pair = TOTAL // PAIR - 1
+            if c == 0:
+                if 0 <= pair - 1 <= last_pair:
+                    turn(pair - 1)
+                if 0 <= pair - 2 <= last_pair:
+                    quantise(pair - 2)
+            else:
+                if 0 <= pair - 1 <= last_pair:
+                    regroup(pair - 1)
+                if 0 <= pair - 2 <= last_pair:
+                    multiply(pair - 2)
+                    if (pair - 2) % (PASSES // PAIR) == PASSES // PAIR - 1:
+                        store((pair - 2) // (PASSES // PAIR))
+
+        with tc.manual_schedule():
             for g in range(TABLE_AHEAD):
-                load_table(table_stage, g)
-            for q in range(PASSES):
+                load_table(g)
+            columns(0)
+            for q in range(NORMALISE_LAG + TOTAL + 3 * PAIR):
                 if q + TABLE_AHEAD < PASSES:
-                    load_table(table_stage, q + TABLE_AHEAD)
-                regroup_table(table_stage, q)
-                if q >= TABLE_LAG:
+                    load_table(q + TABLE_AHEAD)
+                softmax_step(q)
+                if q < PASSES:
+                    regroup_table(q)
+                if 0 <= q - TABLE_LAG < PASSES:
                     quantise_table(q - TABLE_LAG)
-                softmax_step(q)
-            for g in range(PASSES - TABLE_LAG, PASSES):
-                quantise_table(g)
-
-        with tc.tile_pool(name="weight_stage", bufs=2, reuse_waits="tile") as weight_stage:
-            for q in range(SLICES, SLICES * (BATCHES + 1) + NORMALISE_LAG):
-                softmax_step(q)
-                k, rest = divmod(q - NORMALISE_LAG, CHUNK_SLICES)
-                if rest != 0:
-                    continue
-                if 0 <= k < TOTAL_CHUNKS:
-                    normalise(weight_stage, k, (1,))
-                    turn(k)
-                if 0 <= k - 1 < TOTAL_CHUNKS:
-                    regroup(weight_stage, k - 1)
-                if 0 <= k - 2 < TOTAL_CHUNKS:
-                    quantise(weight_stage, k - 2)
-                    multiply(k - 2)
-                    if (k - 2) % CHUNKS == CHUNKS - 1:
-                        store(weight_stage, (k - 2) // CHUNKS)
+                weight_step(q - NORMALISE_LAG, (1,) if q < TOTAL else (1, 3))

@@ -25,22 +25,19 @@ PAIR = 2
 PLANES = 4
 PLANE_ROWS = 4
 RUN = 4
-VECTOR_COLS = 240
 TENSOR_SHARE = 3
 TENSOR_OF = 8
 TENSOR_RESIDUES = [i for i in range(TENSOR_OF) if TENSOR_SHARE * i % TENSOR_OF < TENSOR_SHARE]
 ONES_PARTITION = 32
-TABLE_AHEAD = 3
-TABLE_LAG = 1
-MAX_LAG = 1
-EXP_LAG = 2
-TOP_LAG = 2
-FACTOR_LAG = 3
-TOTAL_LAG = 4
-INVERSE_LAG = 5
-SCALE_LAG = 6
-NORMALISE_LAG = PASSES + SCALE_LAG
-EXP_BUFS = NORMALISE_LAG - EXP_LAG + 3
+STEP = 4
+STEPS = TOTAL // STEP
+ROW_STEPS = PASSES // STEP
+LOAD_AHEAD = 6
+WEIGHT_LAG = ROW_STEPS + 1
+TURN_LAG = WEIGHT_LAG + 1
+QUANTISE_LAG = WEIGHT_LAG + 2
+MULTIPLY_LAG = WEIGHT_LAG + 3
+EXP_BUFS = WEIGHT_LAG * STEP + STEP + 2
 
 FLOPS = 2 * BATCHES * P * VOCAB * DIM
 
@@ -50,10 +47,8 @@ def tile_softembedding_k_kernel(tc, input_numeric, proj_w, proj_b, emb_table, ou
     with ExitStack() as ctx:
         keep = ctx.enter_context(tc.tile_pool(name="keep", bufs=1))
         exp_pool = ctx.enter_context(tc.tile_pool(name="exp_pool", bufs=EXP_BUFS))
-        logit_cols = ctx.enter_context(tc.tile_pool(name="logit_cols", bufs=3))
+        logit_cols = ctx.enter_context(tc.tile_pool(name="logit_cols", bufs=5))
         stats = ctx.enter_context(tc.tile_pool(name="stats", bufs=2))
-        table_stage = ctx.enter_context(tc.tile_pool(name="table_stage", bufs=4))
-        weight_stage = ctx.enter_context(tc.tile_pool(name="weight_stage", bufs=3))
         psum_logit = ctx.enter_context(tc.psum_pool(name="psum_logit", bufs=4))
         psum_turn = ctx.enter_context(tc.psum_pool(name="psum_turn", bufs=3))
         psum_out = ctx.enter_context(tc.psum_pool(name="psum_out", bufs=1))
@@ -82,18 +77,19 @@ def tile_softembedding_k_kernel(tc, input_numeric, proj_w, proj_b, emb_table, ou
         nc.vector.tensor_copy(out=x_rows[:], in_=x_bank[:])
 
         x_pair = keep.tile([P, BATCHES, P], BF16)
-        nc.gpsimd.memset(x_pair[:], 0.0)
-        nc.gpsimd.memset(x_pair[ONES_PARTITION : ONES_PARTITION + 1, :, :], 1.0)
+        nc.vector.memset(x_pair[:], 0.0)
+        nc.vector.memset(x_pair[ONES_PARTITION : ONES_PARTITION + 1, :, :], 1.0)
         nc.sync.dma_start(out=x_pair[0:1, :, :], in_=input_numeric.rearrange("b s o -> o b s"))
-        proj_pair = keep.tile([P, TENSOR_SHARE, PASSES // TENSOR_OF, K_PASS], BF16)
-        nc.gpsimd.memset(proj_pair[:], 0.0)
         w_view = proj_w.rearrange("(q i n) o -> o i q n", i=TENSOR_OF, n=K_PASS)
         b_view = proj_b.rearrange("(o q i n) -> o i q n", o=1, i=TENSOR_OF, n=K_PASS)
+        proj_pair = []
         for slot, residue in enumerate(TENSOR_RESIDUES):
-            nc.sync.dma_start(out=proj_pair[0:1, slot, :, :], in_=w_view[:, residue, :, :])
-            nc.sync.dma_start(
-                out=proj_pair[ONES_PARTITION : ONES_PARTITION + 1, slot, :, :], in_=b_view[:, residue, :, :]
-            )
+            pair = keep.tile([P, PASSES // TENSOR_OF, K_PASS], BF16, name="proj_pair%d" % slot)
+            zero_engine = nc.vector if slot == 0 else nc.gpsimd
+            zero_engine.memset(pair[:].bitcast(F32), 0.0)
+            nc.sync.dma_start(out=pair[0:1, :, :], in_=w_view[:, residue, :, :])
+            nc.sync.dma_start(out=pair[ONES_PARTITION : ONES_PARTITION + 1, :, :], in_=b_view[:, residue, :, :])
+            proj_pair.append(pair)
 
         table_codes = keep.tile([P, PASSES, DIM], U32, align_bytes=64)
         table_scales = keep.tile([P, PASSES // PLANES, DIM], U8, align_bytes=64)
@@ -104,21 +100,26 @@ def tile_softembedding_k_kernel(tc, input_numeric, proj_w, proj_b, emb_table, ou
         table_rows = {}
         table_grouped = {}
 
-        def load_table(g):
-            pass_rows = table_stage.tile([P, PACK, DIM], BF16)
+        def load_table(stage, g):
+            pass_rows = stage.tile([P, PACK, DIM], BF16, bufs=LOAD_AHEAD)
             nc.sync.dma_start(
                 out=pass_rows[:],
                 in_=emb_table[g * K_PASS : (g + 1) * K_PASS, :].rearrange("(p t) d -> p t d", t=PACK),
             )
             table_rows[g] = pass_rows
 
-        def regroup_table(g):
-            pass_grouped = table_stage.tile([P, DIM, PACK], BF16, align_bytes=64)
+        def regroup_table(stage, g, engine, one):
+            pass_grouped = stage.tile([P, DIM, PACK], BF16, align_bytes=64, bufs=6)
             dst = pass_grouped[:].rearrange("p (r i) t -> p r t i", i=RUN)
             src = table_rows[g][:].rearrange("p t (r i) -> p r t i", i=RUN)
-            cut = VECTOR_COLS // RUN
-            nc.vector.tensor_copy(out=dst[:, :cut, :, :], in_=src[:, :cut, :, :])
-            nc.scalar.copy(out=dst[:, cut:, :, :], in_=src[:, cut:, :, :])
+            if engine == "vector":
+                nc.vector.tensor_copy(out=dst, in_=src)
+            elif engine == "scalar":
+                nc.scalar.copy(out=dst, in_=src)
+            else:
+                nc.gpsimd.tensor_scalar(
+                    out=dst, in0=src, scalar1=one[:, 0:1], scalar2=0.0, op0=ALU.mult, op1=ALU.add
+                )
             table_grouped[g] = pass_grouped
 
         def quantise_table(g):
@@ -170,7 +171,7 @@ def tile_softembedding_k_kernel(tc, input_numeric, proj_w, proj_b, emb_table, ou
                 nc.tensor.matmul(
                     out=logit_bank[:],
                     lhsT=x_pair[:, b, :],
-                    rhs=proj_pair[:, TENSOR_RESIDUES.index(i % TENSOR_OF), i // TENSOR_OF, :],
+                    rhs=proj_pair[TENSOR_RESIDUES.index(i % TENSOR_OF)][:, i // TENSOR_OF, :],
                     start=True,
                     stop=True,
                 )
@@ -222,12 +223,17 @@ def tile_softembedding_k_kernel(tc, input_numeric, proj_w, proj_b, emb_table, ou
             nc.vector.reciprocal(out=inv_total[:], in_=inverse[b][:])
             inverse[b] = inv_total
 
-        def row_scales(b):
-            row_slice_scale = stats.tile([P, PASSES], F32)
+        def step_scales(k):
+            b, j = divmod(k, ROW_STEPS)
+            scales = stats.tile([P, STEP], F32)
             nc.vector.tensor_scalar(
-                out=row_slice_scale[:], in0=factors[b][:], scalar1=inverse[b][:, 0:1], scalar2=None, op0=ALU.mult
+                out=scales[:],
+                in0=factors[b][:, STEP * j : STEP * (j + 1)],
+                scalar1=inverse[b][:, 0:1],
+                scalar2=None,
+                op0=ALU.mult,
             )
-            slice_scale[b] = row_slice_scale
+            slice_scale[k] = scales
 
         weights = {}
         turned = {}
@@ -236,19 +242,22 @@ def tile_softembedding_k_kernel(tc, input_numeric, proj_w, proj_b, emb_table, ou
         weight_scales = {}
         acc = {}
 
-        def normalise(m, on_scalar):
-            b, i = divmod(m, PASSES)
+        def normalise(stage, m, engine):
             pair, c = divmod(m, PAIR)
             if c == 0:
-                pair_weights = weight_stage.tile([P, PAIR, 2, P, 2], BF16)
+                pair_weights = stage.tile([P, PAIR, 2, P, 2], BF16, bufs=4)
                 weights[pair] = pair_weights
             target = weights[pair][:, c, :, :, :]
             source = exps[m][:].rearrange("s (p u e) -> s u p e", u=2, e=2)
-            scale = slice_scale[b][:, i : i + 1]
-            if on_scalar:
+            scale = slice_scale[m // STEP][:, m % STEP : m % STEP + 1]
+            if engine == "scalar":
                 nc.scalar.activation(out=target, in_=source, func=ACT.Copy, scale=scale)
-            else:
+            elif engine == "vector":
                 nc.vector.tensor_scalar(out=target, in0=source, scalar1=scale, scalar2=None, op0=ALU.mult)
+            else:
+                nc.gpsimd.tensor_scalar(
+                    out=target, in0=source, scalar1=scale, scalar2=1.0, op0=ALU.mult, op1=ALU.mult
+                )
 
         def turn(pair):
             words = weights[pair][:].rearrange("s c u p e -> s (c u p e)").bitcast(F32)
@@ -259,96 +268,135 @@ def tile_softembedding_k_kernel(tc, input_numeric, proj_w, proj_b, emb_table, ou
                     nc.tensor.transpose(turned_bank[:, c, u, :], words[:, first : first + P], identity[:])
             turned[pair] = turned_bank
 
-        def regroup(pair):
-            pair_grouped = weight_stage.tile([P, PAIR, P, PACK], BF16, align_bytes=64)
-            nc.scalar.copy(out=pair_grouped[:].bitcast(F32), in_=turned[pair][:].rearrange("p c u s -> p c s u"))
-            weight_grouped[pair] = pair_grouped
-
-        def quantise(pair):
-            pair_codes = weight_stage.tile([P, PAIR * P], U32, align_bytes=64)
-            pair_planes = weight_stage.tile([P, PAIR * P], U8, align_bytes=64)
-            nc.vector.quantize_mx(
-                out=pair_codes[:].bitcast(FP8X4),
-                scales=pair_planes[:],
-                in_=weight_grouped[pair][:].rearrange("p c s t -> p (c s t)"),
+        def regroup(stage, pair):
+            k, half = divmod(pair, STEP // PAIR)
+            if half == 0:
+                step_grouped = stage.tile([P, STEP, P, PACK], BF16, align_bytes=64)
+                weight_grouped[k] = step_grouped
+            words = weight_grouped[k][:].bitcast(F32)
+            nc.scalar.copy(
+                out=words[:, PAIR * half : PAIR * (half + 1), :, :],
+                in_=turned[pair][:].rearrange("p c u s -> p c s u"),
             )
-            weight_codes[pair] = pair_codes
-            weight_scales[pair] = pair_planes
 
-        def multiply(pair):
-            b, row_pair = divmod(pair, PASSES // PAIR)
-            if row_pair == 0:
+        def quantise(stage, k):
+            step_codes = stage.tile([P, STEP * P], U32, align_bytes=64)
+            step_planes = stage.tile([P, STEP * P], U8, align_bytes=64)
+            nc.vector.quantize_mx(
+                out=step_codes[:].bitcast(FP8X4),
+                scales=step_planes[:],
+                in_=weight_grouped[k][:].rearrange("p c s t -> p (c s t)"),
+            )
+            weight_codes[k] = step_codes
+            weight_scales[k] = step_planes
+
+        def multiply(k):
+            b, j = divmod(k, ROW_STEPS)
+            if j == 0:
                 row_acc = psum_out.tile([P, DIM], F32)
                 acc[b] = row_acc
-            for c in range(PAIR):
-                g = row_pair * PAIR + c
+            for c in range(STEP):
+                g = j * STEP + c
                 tokens = slice(c * P, (c + 1) * P)
                 nc.tensor.matmul_mx(
                     out=acc[b][:],
-                    lhsT=weight_codes[pair][:, tokens].bitcast(FP8X4),
-                    lhsT_scale=weight_scales[pair][:, tokens],
+                    lhsT=weight_codes[k][:, tokens].bitcast(FP8X4),
+                    lhsT_scale=weight_scales[k][:, tokens],
                     rhs=table_codes[:, g, :].bitcast(FP8X4),
                     rhs_scale=table_plane(g),
                     start=(g == 0),
                     stop=(g == PASSES - 1),
                 )
 
-        def store(b):
-            result = weight_stage.tile([P, DIM], F32)
+        def store(stage, b):
+            result = stage.tile([P, DIM], F32, bufs=1)
             nc.scalar.copy(out=result[:], in_=acc[b][:])
             nc.sync.dma_start(out=out[b], in_=result[:])
 
-        def row_of_last(q):
-            return q // PASSES if 0 <= q < TOTAL and q % PASSES == PASSES - 1 else None
-
-        def softmax_step(q):
-            if q + 1 < TOTAL:
-                columns(q + 1)
-            if q < TOTAL:
-                logits(q)
-            if 0 <= q - MAX_LAG < TOTAL:
-                maximum(q - MAX_LAG)
-            if 0 <= q - EXP_LAG < TOTAL:
-                exponentials(q - EXP_LAG)
-            for lag, stage in (
-                (TOP_LAG, row_top),
-                (FACTOR_LAG, row_factors),
-                (TOTAL_LAG, row_total),
-                (INVERSE_LAG, row_inverse),
-                (SCALE_LAG, row_scales),
-            ):
-                b = row_of_last(q - lag)
-                if b is not None:
-                    stage(b)
-
-        def weight_step(m, scalar_share):
-            pair, c = divmod(m, PAIR)
-            if 0 <= m < TOTAL:
-                normalise(m, m % 4 in scalar_share)
-            last_pair = TOTAL // PAIR - 1
-            if c == 0:
-                if 0 <= pair - 1 <= last_pair:
-                    turn(pair - 1)
-                if 0 <= pair - 2 <= last_pair:
-                    quantise(pair - 2)
-            else:
-                if 0 <= pair - 1 <= last_pair:
-                    regroup(pair - 1)
-                if 0 <= pair - 2 <= last_pair:
-                    multiply(pair - 2)
-                    if (pair - 2) % (PASSES // PAIR) == PASSES // PAIR - 1:
-                        store((pair - 2) // (PASSES // PAIR))
+        def slices_of(k):
+            return range(STEP * k, STEP * (k + 1))
 
         with tc.manual_schedule():
-            for g in range(TABLE_AHEAD):
-                load_table(g)
-            columns(0)
-            for q in range(NORMALISE_LAG + TOTAL + 3 * PAIR):
-                if q + TABLE_AHEAD < PASSES:
-                    load_table(q + TABLE_AHEAD)
-                softmax_step(q)
-                if q < PASSES:
-                    regroup_table(q)
-                if 0 <= q - TABLE_LAG < PASSES:
-                    quantise_table(q - TABLE_LAG)
-                weight_step(q - NORMALISE_LAG, (1,) if q < TOTAL else (1, 3))
+            with tc.tile_pool(name="table_stage", bufs=1) as table_stage:
+                for g in range(LOAD_AHEAD):
+                    load_table(table_stage, g)
+                for q in slices_of(0):
+                    columns(q)
+                for q in slices_of(0):
+                    logits(q)
+                for k in range(ROW_STEPS):
+                    passes = slices_of(k)
+                    one = stats.tile([P, 1], F32)
+                    nc.vector.memset(one[:], 1.0)
+                    regroup_table(table_stage, passes[0], "gpsimd", one)
+                    for q in slices_of(k):
+                        maximum(q)
+                    for q in slices_of(k):
+                        exponentials(q)
+                    for q in slices_of(k + 1):
+                        columns(q)
+                    for q in slices_of(k + 1):
+                        logits(q)
+                    if k >= 1:
+                        for g in slices_of(k - 1):
+                            quantise_table(g)
+                    regroup_table(table_stage, passes[1], "vector", None)
+                    regroup_table(table_stage, passes[2], "scalar", None)
+                    regroup_table(table_stage, passes[3], "scalar", None)
+                    for g in passes:
+                        if g + LOAD_AHEAD < PASSES:
+                            load_table(table_stage, g + LOAD_AHEAD)
+                for g in slices_of(ROW_STEPS - 1):
+                    quantise_table(g)
+
+            with tc.tile_pool(name="weight_stage", bufs=2) as stage:
+                for k in range(ROW_STEPS, STEPS + MULTIPLY_LAG):
+                    row_ends = k % ROW_STEPS == 0
+                    b = k // ROW_STEPS - 1
+                    steady = k < STEPS
+                    kw = k - WEIGHT_LAG
+                    kt = k - TURN_LAG
+                    kq = k - QUANTISE_LAG
+                    km = k - MULTIPLY_LAG
+                    if 0 <= kw < STEPS:
+                        step_scales(kw)
+                        for m in slices_of(kw):
+                            if k <= STEPS:
+                                engine = "gpsimd"
+                            else:
+                                engine = "scalar" if m % STEP == 1 else "vector"
+                            normalise(stage, m, engine)
+                    if row_ends and k <= STEPS:
+                        row_top(b)
+                    if 0 <= kt < STEPS:
+                        turn(2 * kt)
+                        turn(2 * kt + 1)
+                    if 0 <= km < STEPS:
+                        multiply(km)
+                    if steady:
+                        for q in slices_of(k):
+                            maximum(q)
+                    if steady:
+                        exponentials(STEP * k)
+                        exponentials(STEP * k + 1)
+                    if row_ends and k <= STEPS:
+                        row_factors(b)
+                    if 0 <= kt < STEPS:
+                        regroup(stage, 2 * kt)
+                    if steady:
+                        exponentials(STEP * k + 2)
+                        exponentials(STEP * k + 3)
+                    if 0 <= kt < STEPS:
+                        regroup(stage, 2 * kt + 1)
+                    if 0 <= km < STEPS and km % ROW_STEPS == ROW_STEPS - 1:
+                        store(stage, km // ROW_STEPS)
+                    if k + 1 < STEPS:
+                        for q in slices_of(k + 1):
+                            columns(q)
+                        for q in slices_of(k + 1):
+                            logits(q)
+                    if 0 <= kq < STEPS:
+                        quantise(stage, kq)
+                    if row_ends and k <= STEPS:
+                        row_total(b)
+                        row_inverse(b)

@@ -32,6 +32,7 @@ ONES_PARTITION = 32
 STEP = 4
 STEPS = TOTAL // STEP
 ROW_STEPS = PASSES // STEP
+GPSIMD_COLS = 448
 LOAD_AHEAD = 6
 WEIGHT_LAG = ROW_STEPS + 1
 TURN_LAG = WEIGHT_LAG + 1
@@ -112,15 +113,23 @@ def tile_softembedding_k_kernel(tc, input_numeric, proj_w, proj_b, emb_table, ou
             pass_grouped = stage.tile([P, DIM, PACK], BF16, align_bytes=64, bufs=6)
             dst = pass_grouped[:].rearrange("p (r i) t -> p r t i", i=RUN)
             src = table_rows[g][:].rearrange("p t (r i) -> p r t i", i=RUN)
+            table_grouped[g] = pass_grouped
+            if engine == "gpsimd":
+                cut = GPSIMD_COLS // RUN
+                nc.gpsimd.tensor_scalar(
+                    out=dst[:, :cut, :, :],
+                    in0=src[:, :cut, :, :],
+                    scalar1=one[:, 0:1],
+                    scalar2=0.0,
+                    op0=ALU.mult,
+                    op1=ALU.add,
+                )
+                return lambda: nc.vector.tensor_copy(out=dst[:, cut:, :, :], in_=src[:, cut:, :, :])
             if engine == "vector":
                 nc.vector.tensor_copy(out=dst, in_=src)
-            elif engine == "scalar":
-                nc.scalar.copy(out=dst, in_=src)
             else:
-                nc.gpsimd.tensor_scalar(
-                    out=dst, in0=src, scalar1=one[:, 0:1], scalar2=0.0, op0=ALU.mult, op1=ALU.add
-                )
-            table_grouped[g] = pass_grouped
+                nc.scalar.copy(out=dst, in_=src)
+            return None
 
         def quantise_table(g):
             nc.vector.quantize_mx(
@@ -290,12 +299,12 @@ def tile_softembedding_k_kernel(tc, input_numeric, proj_w, proj_b, emb_table, ou
             weight_codes[k] = step_codes
             weight_scales[k] = step_planes
 
-        def multiply(k):
+        def multiply(k, part):
             b, j = divmod(k, ROW_STEPS)
-            if j == 0:
+            if j == 0 and part[0] == 0:
                 row_acc = psum_out.tile([P, DIM], F32)
                 acc[b] = row_acc
-            for c in range(STEP):
+            for c in part:
                 g = j * STEP + c
                 tokens = slice(c * P, (c + 1) * P)
                 nc.tensor.matmul_mx(
@@ -328,7 +337,7 @@ def tile_softembedding_k_kernel(tc, input_numeric, proj_w, proj_b, emb_table, ou
                     passes = slices_of(k)
                     one = stats.tile([P, 1], F32)
                     nc.vector.memset(one[:], 1.0)
-                    regroup_table(table_stage, passes[0], "gpsimd", one)
+                    vector_rest = regroup_table(table_stage, passes[0], "gpsimd", one)
                     for q in slices_of(k):
                         maximum(q)
                     for q in slices_of(k):
@@ -340,6 +349,7 @@ def tile_softembedding_k_kernel(tc, input_numeric, proj_w, proj_b, emb_table, ou
                     if k >= 1:
                         for g in slices_of(k - 1):
                             quantise_table(g)
+                    vector_rest()
                     regroup_table(table_stage, passes[1], "vector", None)
                     regroup_table(table_stage, passes[2], "scalar", None)
                     regroup_table(table_stage, passes[3], "scalar", None)
@@ -362,7 +372,7 @@ def tile_softembedding_k_kernel(tc, input_numeric, proj_w, proj_b, emb_table, ou
                         step_scales(kw)
                         for m in slices_of(kw):
                             if k <= STEPS:
-                                engine = "gpsimd"
+                                engine = "scalar" if m % STEP == STEP - 1 else "gpsimd"
                             else:
                                 engine = "scalar" if m % STEP == 1 else "vector"
                             normalise(stage, m, engine)
@@ -372,7 +382,7 @@ def tile_softembedding_k_kernel(tc, input_numeric, proj_w, proj_b, emb_table, ou
                         turn(2 * kt)
                         turn(2 * kt + 1)
                     if 0 <= km < STEPS:
-                        multiply(km)
+                        multiply(km, (0, 1))
                     if steady:
                         for q in slices_of(k):
                             maximum(q)
@@ -388,13 +398,18 @@ def tile_softembedding_k_kernel(tc, input_numeric, proj_w, proj_b, emb_table, ou
                         exponentials(STEP * k + 3)
                     if 0 <= kt < STEPS:
                         regroup(stage, 2 * kt + 1)
-                    if 0 <= km < STEPS and km % ROW_STEPS == ROW_STEPS - 1:
-                        store(stage, km // ROW_STEPS)
                     if k + 1 < STEPS:
                         for q in slices_of(k + 1):
                             columns(q)
-                        for q in slices_of(k + 1):
-                            logits(q)
+                        logits(STEP * (k + 1))
+                        logits(STEP * (k + 1) + 1)
+                    if 0 <= km < STEPS:
+                        multiply(km, (2, 3))
+                        if km % ROW_STEPS == ROW_STEPS - 1:
+                            store(stage, km // ROW_STEPS)
+                    if k + 1 < STEPS:
+                        logits(STEP * (k + 1) + 2)
+                        logits(STEP * (k + 1) + 3)
                     if 0 <= kq < STEPS:
                         quantise(stage, kq)
                     if row_ends and k <= STEPS:

@@ -197,10 +197,10 @@ def tile_softembedding_k_kernel(tc, input_numeric, proj_w, proj_b, emb_table, ou
 
         def exponentials(q):
             b, i = divmod(q, PASSES)
-            slice_exps = exp_pool.tile([P, K_PASS], F32)
+            slice_exps = exp_pool.tile([P, 2, P, 2], F32)
             nc.scalar.activation(
                 out=slice_exps[:],
-                in_=logit_banks[q][:],
+                in_=logit_banks[q][:].rearrange("s (p u e) -> s u p e", u=2, e=2),
                 func=ACT.Exp,
                 bias=neg_max[b][:, i : i + 1],
                 scale=1.0,
@@ -256,8 +256,8 @@ def tile_softembedding_k_kernel(tc, input_numeric, proj_w, proj_b, emb_table, ou
             if c == 0:
                 pair_weights = stage.tile([P, PAIR, 2, P, 2], BF16, bufs=4)
                 weights[pair] = pair_weights
-            target = weights[pair][:, c, :, :, :]
-            source = exps[m][:].rearrange("s (p u e) -> s u p e", u=2, e=2)
+            target = weights[pair][:, c, :, :, :].rearrange("s u p e -> s (u p e)")
+            source = exps[m][:].rearrange("s u p e -> s (u p e)")
             scale = slice_scale[m // STEP][:, m % STEP : m % STEP + 1]
             if engine == "scalar":
                 nc.scalar.activation(out=target, in_=source, func=ACT.Copy, scale=scale)
@@ -340,6 +340,8 @@ def tile_softembedding_k_kernel(tc, input_numeric, proj_w, proj_b, emb_table, ou
                     vector_rest = regroup_table(table_stage, passes[0], "gpsimd", one)
                     for q in slices_of(k):
                         maximum(q)
+                    if k == 0:
+                        regroup_table(table_stage, passes[2], "scalar", None)
                     for q in slices_of(k):
                         exponentials(q)
                     for q in slices_of(k + 1):
@@ -351,7 +353,8 @@ def tile_softembedding_k_kernel(tc, input_numeric, proj_w, proj_b, emb_table, ou
                             quantise_table(g)
                     vector_rest()
                     regroup_table(table_stage, passes[1], "vector", None)
-                    regroup_table(table_stage, passes[2], "scalar", None)
+                    if k >= 1:
+                        regroup_table(table_stage, passes[2], "scalar", None)
                     regroup_table(table_stage, passes[3], "scalar", None)
                     for g in passes:
                         if g + LOAD_AHEAD < PASSES:
@@ -372,7 +375,7 @@ def tile_softembedding_k_kernel(tc, input_numeric, proj_w, proj_b, emb_table, ou
                         step_scales(kw)
                         for m in slices_of(kw):
                             if k <= STEPS:
-                                engine = "scalar" if m % STEP == STEP - 1 else "gpsimd"
+                                engine = "gpsimd"
                             else:
                                 engine = "scalar" if m % STEP == 1 else "vector"
                             normalise(stage, m, engine)

@@ -117,8 +117,8 @@ def tile_softembedding_k_kernel(tc, input_numeric, proj_w, proj_b, emb_table, ou
             if engine == "gpsimd":
                 cut = GPSIMD_COLS // RUN
                 nc.gpsimd.tensor_scalar(
-                    out=dst[:, :cut, :, :],
-                    in0=src[:, :cut, :, :],
+                    out=pass_grouped[:, :GPSIMD_COLS, :],
+                    in0=table_rows[g][:, :, :GPSIMD_COLS].rearrange("p t d -> p d t"),
                     scalar1=one[:, 0:1],
                     scalar2=0.0,
                     op0=ALU.mult,
@@ -375,7 +375,7 @@ def tile_softembedding_k_kernel(tc, input_numeric, proj_w, proj_b, emb_table, ou
                         step_scales(kw)
                         for m in slices_of(kw):
                             if k <= STEPS:
-                                engine = "gpsimd"
+                                engine = "scalar" if m % STEP == STEP - 1 else "gpsimd"
                             else:
                                 engine = "scalar" if m % STEP == 1 else "vector"
                             normalise(stage, m, engine)

@@ -38,7 +38,8 @@ WEIGHT_LAG = ROW_STEPS + 1
 TURN_LAG = WEIGHT_LAG + 1
 QUANTISE_LAG = WEIGHT_LAG + 2
 MULTIPLY_LAG = WEIGHT_LAG + 3
-EXP_BUFS = WEIGHT_LAG * STEP + STEP + 2
+EXP_BUFS = WEIGHT_LAG + 1
+SCALAR_COLUMNS = 1
 
 FLOPS = 2 * BATCHES * P * VOCAB * DIM
 
@@ -139,6 +140,7 @@ def tile_softembedding_k_kernel(tc, input_numeric, proj_w, proj_b, emb_table, ou
             )
 
         slice_cols = {}
+        slice_max = {}
         logit_banks = {}
         exps = {}
         neg_max = {}
@@ -151,17 +153,18 @@ def tile_softembedding_k_kernel(tc, input_numeric, proj_w, proj_b, emb_table, ou
         def by_tensor(q):
             return q % TENSOR_OF in TENSOR_RESIDUES
 
-        def columns(q):
+        def columns(q, scalar_share):
             b, i = divmod(q, PASSES)
             if i == 0:
-                row_neg_max = stats.tile([P, PASSES], F32)
-                row_part_sum = stats.tile([P, PASSES], F32)
+                row_neg_max = stats.tile([P, ROW_STEPS], F32)
+                row_part_sum = stats.tile([P, ROW_STEPS], F32)
                 neg_max[b] = row_neg_max
                 part_sum[b] = row_part_sum
             if by_tensor(q):
                 return
             cols = logit_cols.tile([P, COLS, P], F32)
-            for c in range(COLS):
+            slice_cols[q] = cols
+            for c in range(COLS - scalar_share):
                 a = COLS * i + c
                 nc.vector.tensor_scalar(
                     out=cols[:, c, :],
@@ -171,7 +174,20 @@ def tile_softembedding_k_kernel(tc, input_numeric, proj_w, proj_b, emb_table, ou
                     op0=ALU.mult,
                     op1=ALU.add,
                 )
-            slice_cols[q] = cols
+
+        def scalar_columns(q, scalar_share):
+            b, i = divmod(q, PASSES)
+            if by_tensor(q):
+                return
+            for c in range(COLS - scalar_share, COLS):
+                a = COLS * i + c
+                nc.scalar.activation(
+                    out=slice_cols[q][:, c, :],
+                    in_=x_rows[:, b, :],
+                    func=ACT.Identity,
+                    scale=proj_cols[:, 0, a : a + 1],
+                    bias=proj_cols[:, 1, a : a + 1],
+                )
 
         def logits(q):
             b, i = divmod(q, PASSES)
@@ -189,24 +205,39 @@ def tile_softembedding_k_kernel(tc, input_numeric, proj_w, proj_b, emb_table, ou
                     nc.tensor.transpose(logit_bank[:, c * P : (c + 1) * P], slice_cols[q][:, c, :], identity[:])
             logit_banks[q] = logit_bank
 
-        def maximum(q):
-            b, i = divmod(q, PASSES)
+        def collect(k):
+            step_exps = exp_pool.tile([P, STEP, K_PASS], F32)
+            step_max = stats.tile([P, STEP], F32)
+            for c in range(STEP):
+                nc.vector.tensor_scalar(
+                    out=step_exps[:, c, :].rearrange("s (u p e) -> s u p e", u=2, e=2),
+                    in0=logit_banks[STEP * k + c][:].rearrange("s (p u e) -> s u p e", u=2, e=2),
+                    scalar1=0.0,
+                    scalar2=None,
+                    op0=ALU.add,
+                    op1=ALU.max,
+                    accum_out=step_max[:, c : c + 1],
+                )
+            exps[k] = step_exps
+            slice_max[k] = step_max
+
+        def maximum(k):
+            b, j = divmod(k, ROW_STEPS)
             nc.vector.tensor_reduce(
-                out=neg_max[b][:, i : i + 1], in_=logit_banks[q][:], axis=AXIS.X, op=ALU.max, negate=True
+                out=neg_max[b][:, j : j + 1], in_=slice_max[k][:], axis=AXIS.X, op=ALU.max, negate=True
             )
 
-        def exponentials(q):
-            b, i = divmod(q, PASSES)
-            slice_exps = exp_pool.tile([P, 2, P, 2], F32)
+        def exponentials(k):
+            b, j = divmod(k, ROW_STEPS)
+            logits_and_exps = exps[k][:].rearrange("s c n -> s (c n)")
             nc.scalar.activation(
-                out=slice_exps[:],
-                in_=logit_banks[q][:].rearrange("s (p u e) -> s u p e", u=2, e=2),
+                out=logits_and_exps,
+                in_=logits_and_exps,
                 func=ACT.Exp,
-                bias=neg_max[b][:, i : i + 1],
+                bias=neg_max[b][:, j : j + 1],
                 scale=1.0,
-                accum_out=part_sum[b][:, i : i + 1],
+                accum_out=part_sum[b][:, j : j + 1],
             )
-            exps[q] = slice_exps
 
         def row_top(b):
             top = stats.tile([P, 1], F32)
@@ -214,14 +245,14 @@ def tile_softembedding_k_kernel(tc, input_numeric, proj_w, proj_b, emb_table, ou
             neg_top[b] = top
 
         def row_factors(b):
-            factor = stats.tile([P, PASSES], F32)
+            factor = stats.tile([P, ROW_STEPS], F32)
             nc.scalar.activation(
                 out=factor[:], in_=neg_max[b][:], func=ACT.Exp, bias=neg_top[b][:, 0:1], scale=-1.0
             )
             factors[b] = factor
 
         def row_total(b):
-            weighted = stats.tile([P, PASSES], F32)
+            weighted = stats.tile([P, ROW_STEPS], F32)
             nc.vector.tensor_tensor(out=weighted[:], in0=factors[b][:], in1=part_sum[b][:], op=ALU.mult)
             total = stats.tile([P, 1], F32)
             nc.vector.tensor_reduce(out=total[:], in_=weighted[:], axis=AXIS.X, op=ALU.add)
@@ -234,10 +265,10 @@ def tile_softembedding_k_kernel(tc, input_numeric, proj_w, proj_b, emb_table, ou
 
         def step_scales(k):
             b, j = divmod(k, ROW_STEPS)
-            scales = stats.tile([P, STEP], F32)
+            scales = stats.tile([P, 1], F32)
             nc.vector.tensor_scalar(
                 out=scales[:],
-                in0=factors[b][:, STEP * j : STEP * (j + 1)],
+                in0=factors[b][:, j : j + 1],
                 scalar1=inverse[b][:, 0:1],
                 scalar2=None,
                 op0=ALU.mult,
@@ -251,14 +282,14 @@ def tile_softembedding_k_kernel(tc, input_numeric, proj_w, proj_b, emb_table, ou
         weight_scales = {}
         acc = {}
 
-        def normalise(stage, m, engine):
-            pair, c = divmod(m, PAIR)
-            if c == 0:
-                pair_weights = stage.tile([P, PAIR, 2, P, 2], BF16, bufs=4)
-                weights[pair] = pair_weights
-            target = weights[pair][:, c, :, :, :].rearrange("s u p e -> s (u p e)")
-            source = exps[m][:].rearrange("s u p e -> s (u p e)")
-            scale = slice_scale[m // STEP][:, m % STEP : m % STEP + 1]
+        def weight_tile(stage, k):
+            step_weights = stage.tile([P, STEP, K_PASS], BF16)
+            weights[k] = step_weights
+
+        def normalise(k, first, last, engine):
+            target = weights[k][:, first:last, :].rearrange("s c n -> s (c n)")
+            source = exps[k][:, first:last, :].rearrange("s c n -> s (c n)")
+            scale = slice_scale[k][:, 0:1]
             if engine == "scalar":
                 nc.scalar.activation(out=target, in_=source, func=ACT.Copy, scale=scale)
             elif engine == "vector":
@@ -269,11 +300,12 @@ def tile_softembedding_k_kernel(tc, input_numeric, proj_w, proj_b, emb_table, ou
                 )
 
         def turn(pair):
-            words = weights[pair][:].rearrange("s c u p e -> s (c u p e)").bitcast(F32)
+            k, half = divmod(pair, STEP // PAIR)
+            words = weights[k][:].rearrange("s c n -> s (c n)").bitcast(F32)
             turned_bank = psum_turn.tile([P, PAIR, 2, P], F32, tag="turn_bank")
             for c in range(PAIR):
                 for u in range(2):
-                    first = (2 * c + u) * P
+                    first = (2 * (PAIR * half + c) + u) * P
                     nc.tensor.transpose(turned_bank[:, c, u, :], words[:, first : first + P], identity[:])
             turned[pair] = turned_bank
 
@@ -330,7 +362,7 @@ def tile_softembedding_k_kernel(tc, input_numeric, proj_w, proj_b, emb_table, ou
                 for g in range(LOAD_AHEAD):
                     load_table(table_stage, g)
                 for q in slices_of(0):
-                    columns(q)
+                    columns(q, 0)
                 for q in slices_of(0):
                     logits(q)
                 for k in range(ROW_STEPS):
@@ -338,14 +370,13 @@ def tile_softembedding_k_kernel(tc, input_numeric, proj_w, proj_b, emb_table, ou
                     one = stats.tile([P, 1], F32)
                     nc.vector.memset(one[:], 1.0)
                     vector_rest = regroup_table(table_stage, passes[0], "gpsimd", one)
-                    for q in slices_of(k):
-                        maximum(q)
+                    collect(k)
                     if k == 0:
                         regroup_table(table_stage, passes[2], "scalar", None)
-                    for q in slices_of(k):
-                        exponentials(q)
                     for q in slices_of(k + 1):
-                        columns(q)
+                        columns(q, 0)
+                    maximum(k)
+                    exponentials(k)
                     for q in slices_of(k + 1):
                         logits(q)
                     if k >= 1:
@@ -364,57 +395,57 @@ def tile_softembedding_k_kernel(tc, input_numeric, proj_w, proj_b, emb_table, ou
 
             with tc.tile_pool(name="weight_stage", bufs=2) as stage:
                 for k in range(ROW_STEPS, STEPS + MULTIPLY_LAG):
-                    row_ends = k % ROW_STEPS == 0
+                    row_ends = k % ROW_STEPS == 0 and k <= STEPS
                     b = k // ROW_STEPS - 1
-                    steady = k < STEPS
+                    soft = k < STEPS
                     kw = k - WEIGHT_LAG
                     kt = k - TURN_LAG
                     kq = k - QUANTISE_LAG
                     km = k - MULTIPLY_LAG
+                    has_next = k + 1 < STEPS
                     if 0 <= kw < STEPS:
                         step_scales(kw)
-                        for m in slices_of(kw):
-                            if k <= STEPS:
-                                engine = "scalar" if m % STEP == STEP - 1 else "gpsimd"
-                            else:
-                                engine = "scalar" if m % STEP == 1 else "vector"
-                            normalise(stage, m, engine)
-                    if row_ends and k <= STEPS:
+                        weight_tile(stage, kw)
+                        if k <= STEPS:
+                            normalise(kw, 0, STEP, "gpsimd")
+                        else:
+                            normalise(kw, 0, 1, "scalar")
+                            normalise(kw, 1, STEP, "vector")
+                    if row_ends:
                         row_top(b)
                     if 0 <= kt < STEPS:
                         turn(2 * kt)
                         turn(2 * kt + 1)
                     if 0 <= km < STEPS:
                         multiply(km, (0, 1))
-                    if steady:
-                        for q in slices_of(k):
-                            maximum(q)
-                    if steady:
-                        exponentials(STEP * k)
-                        exponentials(STEP * k + 1)
-                    if row_ends and k <= STEPS:
+                    if soft:
+                        collect(k)
+                    if row_ends:
                         row_factors(b)
                     if 0 <= kt < STEPS:
                         regroup(stage, 2 * kt)
-                    if steady:
-                        exponentials(STEP * k + 2)
-                        exponentials(STEP * k + 3)
+                    if has_next:
+                        for q in slices_of(k + 1):
+                            columns(q, SCALAR_COLUMNS)
+                        for q in slices_of(k + 1):
+                            scalar_columns(q, SCALAR_COLUMNS)
                     if 0 <= kt < STEPS:
                         regroup(stage, 2 * kt + 1)
-                    if k + 1 < STEPS:
-                        for q in slices_of(k + 1):
-                            columns(q)
+                    if soft:
+                        maximum(k)
+                        exponentials(k)
+                    if has_next:
                         logits(STEP * (k + 1))
                         logits(STEP * (k + 1) + 1)
                     if 0 <= km < STEPS:
                         multiply(km, (2, 3))
                         if km % ROW_STEPS == ROW_STEPS - 1:
                             store(stage, km // ROW_STEPS)
-                    if k + 1 < STEPS:
+                    if has_next:
                         logits(STEP * (k + 1) + 2)
                         logits(STEP * (k + 1) + 3)
                     if 0 <= kq < STEPS:
                         quantise(stage, kq)
-                    if row_ends and k <= STEPS:
+                    if row_ends:
                         row_total(b)
                         row_inverse(b)

@@ -33,7 +33,7 @@ STEP = 4
 STEPS = TOTAL // STEP
 ROW_STEPS = PASSES // STEP
 GPSIMD_COLS = 448
-LOAD_AHEAD = 6
+LOAD_AHEAD = 8
 WEIGHT_LAG = ROW_STEPS + 1
 TURN_LAG = WEIGHT_LAG + 1
 QUANTISE_LAG = WEIGHT_LAG + 2
@@ -55,12 +55,12 @@ def tile_softembedding_k_kernel(tc, input_numeric, proj_w, proj_b, emb_table, ou
         psum_turn = ctx.enter_context(tc.psum_pool(name="psum_turn", bufs=3))
         psum_out = ctx.enter_context(tc.psum_pool(name="psum_out", bufs=1))
 
-        proj_loaded = keep.tile([P, 2, P], BF16)
-        nc.sync.dma_start(out=proj_loaded[:, 0, :], in_=proj_w.rearrange("(a p) o -> a (p o)", p=P))
-        nc.sync.dma_start(out=proj_loaded[:, 1, :], in_=proj_b.rearrange("(a p) -> a p", p=P))
         x_bf = keep.tile([P, BATCHES], BF16)
         with nc.allow_non_contiguous_dma(reason="512 scalars, one token to a partition"):
             nc.sync.dma_start(out=x_bf[:], in_=input_numeric.rearrange("b s o -> s (b o)"))
+        proj_loaded = keep.tile([P, 2, P], BF16)
+        nc.sync.dma_start(out=proj_loaded[:, 0, :], in_=proj_w.rearrange("(a p) o -> a (p o)", p=P))
+        nc.sync.dma_start(out=proj_loaded[:, 1, :], in_=proj_b.rearrange("(a p) -> a p", p=P))
 
         identity_bf = keep.tile([P, P], BF16)
         make_identity(nc, identity_bf[:])
@@ -125,7 +125,7 @@ def tile_softembedding_k_kernel(tc, input_numeric, proj_w, proj_b, emb_table, ou
                     op0=ALU.mult,
                     op1=ALU.add,
                 )
-                return lambda: nc.vector.tensor_copy(out=dst[:, cut:, :, :], in_=src[:, cut:, :, :])
+                return lambda: nc.scalar.copy(out=dst[:, cut:, :, :], in_=src[:, cut:, :, :])
             if engine == "vector":
                 nc.vector.tensor_copy(out=dst, in_=src)
             else:
@@ -148,7 +148,7 @@ def tile_softembedding_k_kernel(tc, input_numeric, proj_w, proj_b, emb_table, ou
         neg_top = {}
         factors = {}
         inverse = {}
-        slice_scale = {}
+        row_scale = {}
 
         def by_tensor(q):
             return q % TENSOR_OF in TENSOR_RESIDUES
@@ -205,13 +205,18 @@ def tile_softembedding_k_kernel(tc, input_numeric, proj_w, proj_b, emb_table, ou
                     nc.tensor.transpose(logit_bank[:, c * P : (c + 1) * P], slice_cols[q][:, c, :], identity[:])
             logit_banks[q] = logit_bank
 
+        def fill_order(k):
+            slices = range(STEP * k, STEP * (k + 1))
+            return [q for q in slices if by_tensor(q)] + [q for q in slices if not by_tensor(q)]
+
         def collect(k):
             step_exps = exp_pool.tile([P, STEP, K_PASS], F32)
             step_max = stats.tile([P, STEP], F32)
-            for c in range(STEP):
+            for q in fill_order(k):
+                c = q - STEP * k
                 nc.vector.tensor_scalar(
                     out=step_exps[:, c, :].rearrange("s (u p e) -> s u p e", u=2, e=2),
-                    in0=logit_banks[STEP * k + c][:].rearrange("s (p u e) -> s u p e", u=2, e=2),
+                    in0=logit_banks[q][:].rearrange("s (p u e) -> s u p e", u=2, e=2),
                     scalar1=0.0,
                     scalar2=None,
                     op0=ALU.add,
@@ -253,9 +258,16 @@ def tile_softembedding_k_kernel(tc, input_numeric, proj_w, proj_b, emb_table, ou
 
         def row_total(b):
             weighted = stats.tile([P, ROW_STEPS], F32)
-            nc.vector.tensor_tensor(out=weighted[:], in0=factors[b][:], in1=part_sum[b][:], op=ALU.mult)
             total = stats.tile([P, 1], F32)
-            nc.vector.tensor_reduce(out=total[:], in_=weighted[:], axis=AXIS.X, op=ALU.add)
+            nc.vector.scalar_tensor_tensor(
+                out=weighted[:],
+                in0=factors[b][:],
+                scalar=1.0,
+                in1=part_sum[b][:],
+                op0=ALU.mult,
+                op1=ALU.mult,
+                accum_out=total[:],
+            )
             inverse[b] = total
 
         def row_inverse(b):
@@ -263,17 +275,12 @@ def tile_softembedding_k_kernel(tc, input_numeric, proj_w, proj_b, emb_table, ou
             nc.vector.reciprocal(out=inv_total[:], in_=inverse[b][:])
             inverse[b] = inv_total
 
-        def step_scales(k):
-            b, j = divmod(k, ROW_STEPS)
-            scales = stats.tile([P, 1], F32)
+        def row_scales(b):
+            scales = stats.tile([P, ROW_STEPS], F32)
             nc.vector.tensor_scalar(
-                out=scales[:],
-                in0=factors[b][:, j : j + 1],
-                scalar1=inverse[b][:, 0:1],
-                scalar2=None,
-                op0=ALU.mult,
+                out=scales[:], in0=factors[b][:], scalar1=inverse[b][:, 0:1], scalar2=None, op0=ALU.mult
             )
-            slice_scale[k] = scales
+            row_scale[b] = scales
 
         weights = {}
         turned = {}
@@ -286,17 +293,16 @@ def tile_softembedding_k_kernel(tc, input_numeric, proj_w, proj_b, emb_table, ou
             step_weights = stage.tile([P, STEP, K_PASS], BF16)
             weights[k] = step_weights
 
-        def normalise(k, first, last, engine):
-            target = weights[k][:, first:last, :].rearrange("s c n -> s (c n)")
-            source = exps[k][:, first:last, :].rearrange("s c n -> s (c n)")
-            scale = slice_scale[k][:, 0:1]
-            if engine == "scalar":
-                nc.scalar.activation(out=target, in_=source, func=ACT.Copy, scale=scale)
-            elif engine == "vector":
+        def normalise(k, one):
+            b, j = divmod(k, ROW_STEPS)
+            target = weights[k][:].rearrange("s c n -> s (c n)")
+            source = exps[k][:].rearrange("s c n -> s (c n)")
+            scale = row_scale[b][:, j : j + 1]
+            if one is None:
                 nc.vector.tensor_scalar(out=target, in0=source, scalar1=scale, scalar2=None, op0=ALU.mult)
             else:
                 nc.gpsimd.tensor_scalar(
-                    out=target, in0=source, scalar1=scale, scalar2=1.0, op0=ALU.mult, op1=ALU.mult
+                    out=target, in0=source, scalar1=scale, scalar2=one[:, 0:1], op0=ALU.mult, op1=ALU.mult
                 )
 
         def turn(pair):
@@ -320,16 +326,19 @@ def tile_softembedding_k_kernel(tc, input_numeric, proj_w, proj_b, emb_table, ou
                 in_=turned[pair][:].rearrange("p c u s -> p c s u"),
             )
 
-        def quantise(stage, k):
+        def code_tiles(stage, k):
             step_codes = stage.tile([P, STEP * P], U32, align_bytes=64)
             step_planes = stage.tile([P, STEP * P], U8, align_bytes=64)
-            nc.vector.quantize_mx(
-                out=step_codes[:].bitcast(FP8X4),
-                scales=step_planes[:],
-                in_=weight_grouped[k][:].rearrange("p c s t -> p (c s t)"),
-            )
             weight_codes[k] = step_codes
             weight_scales[k] = step_planes
+
+        def quantise(k, first, last):
+            tokens = slice(first * P, last * P)
+            nc.vector.quantize_mx(
+                out=weight_codes[k][:, tokens].bitcast(FP8X4),
+                scales=weight_scales[k][:, tokens],
+                in_=weight_grouped[k][:, first:last, :, :].rearrange("p c s t -> p (c s t)"),
+            )
 
         def multiply(k, part):
             b, j = divmod(k, ROW_STEPS)
@@ -359,17 +368,17 @@ def tile_softembedding_k_kernel(tc, input_numeric, proj_w, proj_b, emb_table, ou
 
         with tc.manual_schedule():
             with tc.tile_pool(name="table_stage", bufs=1) as table_stage:
-                for g in range(LOAD_AHEAD):
+                for g in [2, 0, 1] + list(range(3, LOAD_AHEAD)):
                     load_table(table_stage, g)
                 for q in slices_of(0):
                     columns(q, 0)
-                for q in slices_of(0):
+                for q in fill_order(0):
                     logits(q)
                 for k in range(ROW_STEPS):
                     passes = slices_of(k)
                     one = stats.tile([P, 1], F32)
                     nc.vector.memset(one[:], 1.0)
-                    vector_rest = regroup_table(table_stage, passes[0], "gpsimd", one)
+                    scalar_rest = regroup_table(table_stage, passes[0], "gpsimd", one)
                     collect(k)
                     if k == 0:
                         regroup_table(table_stage, passes[2], "scalar", None)
@@ -377,12 +386,12 @@ def tile_softembedding_k_kernel(tc, input_numeric, proj_w, proj_b, emb_table, ou
                         columns(q, 0)
                     maximum(k)
                     exponentials(k)
-                    for q in slices_of(k + 1):
+                    for q in fill_order(k + 1):
                         logits(q)
                     if k >= 1:
                         for g in slices_of(k - 1):
                             quantise_table(g)
-                    vector_rest()
+                    scalar_rest()
                     regroup_table(table_stage, passes[1], "vector", None)
                     if k >= 1:
                         regroup_table(table_stage, passes[2], "scalar", None)
@@ -394,7 +403,8 @@ def tile_softembedding_k_kernel(tc, input_numeric, proj_w, proj_b, emb_table, ou
                     quantise_table(g)
 
             with tc.tile_pool(name="weight_stage", bufs=2) as stage:
-                for k in range(ROW_STEPS, STEPS + MULTIPLY_LAG):
+                last = STEPS - 1
+                for k in range(ROW_STEPS, last + QUANTISE_LAG):
                     row_ends = k % ROW_STEPS == 0 and k <= STEPS
                     b = k // ROW_STEPS - 1
                     soft = k < STEPS
@@ -404,18 +414,19 @@ def tile_softembedding_k_kernel(tc, input_numeric, proj_w, proj_b, emb_table, ou
                     km = k - MULTIPLY_LAG
                     has_next = k + 1 < STEPS
                     if 0 <= kw < STEPS:
-                        step_scales(kw)
                         weight_tile(stage, kw)
+                        one = None
                         if k <= STEPS:
-                            normalise(kw, 0, STEP, "gpsimd")
-                        else:
-                            normalise(kw, 0, 1, "scalar")
-                            normalise(kw, 1, STEP, "vector")
+                            one = stats.tile([P, 1], F32)
+                            nc.vector.memset(one[:], 1.0)
+                        normalise(kw, one)
                     if row_ends:
                         row_top(b)
                     if 0 <= kt < STEPS:
                         turn(2 * kt)
                         turn(2 * kt + 1)
+                    if kt == last:
+                        code_tiles(stage, last)
                     if 0 <= km < STEPS:
                         multiply(km, (0, 1))
                     if soft:
@@ -424,28 +435,37 @@ def tile_softembedding_k_kernel(tc, input_numeric, proj_w, proj_b, emb_table, ou
                         row_factors(b)
                     if 0 <= kt < STEPS:
                         regroup(stage, 2 * kt)
+                    tasks = [row_total, row_inverse, row_scales] if row_ends else []
                     if has_next:
                         for q in slices_of(k + 1):
+                            if tasks:
+                                tasks.pop(0)(b)
                             columns(q, SCALAR_COLUMNS)
                         for q in slices_of(k + 1):
                             scalar_columns(q, SCALAR_COLUMNS)
+                    for task in tasks:
+                        task(b)
                     if 0 <= kt < STEPS:
                         regroup(stage, 2 * kt + 1)
                     if soft:
                         maximum(k)
                         exponentials(k)
-                    if has_next:
-                        logits(STEP * (k + 1))
-                        logits(STEP * (k + 1) + 1)
+                    fills = fill_order(k + 1) if has_next else []
+                    for q in fills[:2]:
+                        logits(q)
                     if 0 <= km < STEPS:
                         multiply(km, (2, 3))
                         if km % ROW_STEPS == ROW_STEPS - 1:
                             store(stage, km // ROW_STEPS)
-                    if has_next:
-                        logits(STEP * (k + 1) + 2)
-                        logits(STEP * (k + 1) + 3)
-                    if 0 <= kq < STEPS:
-                        quantise(stage, kq)
-                    if row_ends:
-                        row_total(b)
-                        row_inverse(b)
+                    for q in fills[2:]:
+                        logits(q)
+                    if 0 <= kq < last:
+                        code_tiles(stage, kq)
+                        quantise(kq, 0, STEP)
+                    if kt == last:
+                        quantise(last, 0, PAIR)
+                        quantise(last, PAIR, STEP)
+                multiply(last - 1, range(STEP))
+                multiply(last, (0, 1))
+                multiply(last, (2, 3))
+                store(stage, BATCHES - 1)

@@ -32,14 +32,13 @@ ONES_PARTITION = 32
 STEP = 4
 STEPS = TOTAL // STEP
 ROW_STEPS = PASSES // STEP
-GPSIMD_COLS = 448
 LOAD_AHEAD = 8
 WEIGHT_LAG = ROW_STEPS + 1
 TURN_LAG = WEIGHT_LAG + 1
 QUANTISE_LAG = WEIGHT_LAG + 2
 MULTIPLY_LAG = WEIGHT_LAG + 3
 EXP_BUFS = WEIGHT_LAG + 1
-SCALAR_COLUMNS = 1
+HEAD_SCALAR_COLUMNS = 1
 
 FLOPS = 2 * BATCHES * P * VOCAB * DIM
 
@@ -87,7 +86,7 @@ def tile_softembedding_k_kernel(tc, input_numeric, proj_w, proj_b, emb_table, ou
         proj_pair = []
         for slot, residue in enumerate(TENSOR_RESIDUES):
             pair = keep.tile([P, PASSES // TENSOR_OF, K_PASS], BF16, name="proj_pair%d" % slot)
-            zero_engine = nc.vector if slot == 0 else nc.gpsimd
+            zero_engine = nc.gpsimd if slot == TENSOR_SHARE - 1 else nc.vector
             zero_engine.memset(pair[:].bitcast(F32), 0.0)
             nc.sync.dma_start(out=pair[0:1, :, :], in_=w_view[:, residue, :, :])
             nc.sync.dma_start(out=pair[ONES_PARTITION : ONES_PARTITION + 1, :, :], in_=b_view[:, residue, :, :])
@@ -116,21 +115,18 @@ def tile_softembedding_k_kernel(tc, input_numeric, proj_w, proj_b, emb_table, ou
             src = table_rows[g][:].rearrange("p t (r i) -> p r t i", i=RUN)
             table_grouped[g] = pass_grouped
             if engine == "gpsimd":
-                cut = GPSIMD_COLS // RUN
                 nc.gpsimd.tensor_scalar(
-                    out=pass_grouped[:, :GPSIMD_COLS, :],
-                    in0=table_rows[g][:, :, :GPSIMD_COLS].rearrange("p t d -> p d t"),
+                    out=pass_grouped[:],
+                    in0=table_rows[g][:].rearrange("p t d -> p d t"),
                     scalar1=one[:, 0:1],
                     scalar2=0.0,
                     op0=ALU.mult,
                     op1=ALU.add,
                 )
-                return lambda: nc.scalar.copy(out=dst[:, cut:, :, :], in_=src[:, cut:, :, :])
-            if engine == "vector":
+            elif engine == "vector":
                 nc.vector.tensor_copy(out=dst, in_=src)
             else:
                 nc.scalar.copy(out=dst, in_=src)
-            return None
 
         def quantise_table(g):
             nc.vector.quantize_mx(
@@ -378,12 +374,14 @@ def tile_softembedding_k_kernel(tc, input_numeric, proj_w, proj_b, emb_table, ou
                     passes = slices_of(k)
                     one = stats.tile([P, 1], F32)
                     nc.vector.memset(one[:], 1.0)
-                    scalar_rest = regroup_table(table_stage, passes[0], "gpsimd", one)
+                    regroup_table(table_stage, passes[0], "gpsimd", one)
                     collect(k)
                     if k == 0:
                         regroup_table(table_stage, passes[2], "scalar", None)
                     for q in slices_of(k + 1):
-                        columns(q, 0)
+                        columns(q, HEAD_SCALAR_COLUMNS)
+                    for q in slices_of(k + 1):
+                        scalar_columns(q, HEAD_SCALAR_COLUMNS)
                     maximum(k)
                     exponentials(k)
                     for q in fill_order(k + 1):
@@ -391,7 +389,6 @@ def tile_softembedding_k_kernel(tc, input_numeric, proj_w, proj_b, emb_table, ou
                     if k >= 1:
                         for g in slices_of(k - 1):
                             quantise_table(g)
-                    scalar_rest()
                     regroup_table(table_stage, passes[1], "vector", None)
                     if k >= 1:
                         regroup_table(table_stage, passes[2], "scalar", None)
@@ -440,9 +437,9 @@ def tile_softembedding_k_kernel(tc, input_numeric, proj_w, proj_b, emb_table, ou
                         for q in slices_of(k + 1):
                             if tasks:
                                 tasks.pop(0)(b)
-                            columns(q, SCALAR_COLUMNS)
+                            columns(q, 1 + q % 2)
                         for q in slices_of(k + 1):
-                            scalar_columns(q, SCALAR_COLUMNS)
+                            scalar_columns(q, 1 + q % 2)
                     for task in tasks:
                         task(b)
                     if 0 <= kt < STEPS:

@@ -28,6 +28,7 @@ RUN = 4
 TENSOR_SHARE = 3
 TENSOR_OF = 8
 TENSOR_RESIDUES = [i for i in range(TENSOR_OF) if TENSOR_SHARE * i % TENSOR_OF < TENSOR_SHARE]
+LAST_PASS_ROWS = 3
 ONES_PARTITION = 32
 STEP = 4
 STEPS = TOTAL // STEP
@@ -38,6 +39,7 @@ TURN_LAG = WEIGHT_LAG + 1
 QUANTISE_LAG = WEIGHT_LAG + 2
 MULTIPLY_LAG = WEIGHT_LAG + 3
 EXP_BUFS = WEIGHT_LAG + 1
+VECTOR_WEIGHTS = 1792
 HEAD_SCALAR_COLUMNS = 1
 
 FLOPS = 2 * BATCHES * P * VOCAB * DIM
@@ -51,8 +53,10 @@ def tile_softembedding_k_kernel(tc, input_numeric, proj_w, proj_b, emb_table, ou
         logit_cols = ctx.enter_context(tc.tile_pool(name="logit_cols", bufs=5))
         stats = ctx.enter_context(tc.tile_pool(name="stats", bufs=2))
         psum_logit = ctx.enter_context(tc.psum_pool(name="psum_logit", bufs=4))
-        psum_turn = ctx.enter_context(tc.psum_pool(name="psum_turn", bufs=3))
-        psum_out = ctx.enter_context(tc.psum_pool(name="psum_out", bufs=1))
+        psum_turn = ctx.enter_context(tc.psum_pool(name="psum_turn", bufs=2))
+        psum_out = ctx.enter_context(tc.psum_pool(name="psum_out", bufs=2))
+
+        ctx.enter_context(tc.manual_schedule())
 
         x_bf = keep.tile([P, BATCHES], BF16)
         with nc.allow_non_contiguous_dma(reason="512 scalars, one token to a partition"):
@@ -66,17 +70,6 @@ def tile_softembedding_k_kernel(tc, input_numeric, proj_w, proj_b, emb_table, ou
         identity = keep.tile([P, P], F32)
         make_identity(nc, identity[:])
 
-        head_bank = psum_out.tile([P, 2, P], BF16, tag="row_acc")
-        nc.tensor.transpose(head_bank[:, 0, :], proj_loaded[:, 0, :], identity_bf[:])
-        nc.tensor.transpose(head_bank[:, 1, :], proj_loaded[:, 1, :], identity_bf[:])
-        proj_cols = keep.tile([P, 2, P], F32)
-        nc.vector.tensor_copy(out=proj_cols[:], in_=head_bank[:])
-        x_bank = psum_turn.tile([P, BATCHES, P], BF16, tag="turn_bank")
-        for b in range(BATCHES):
-            nc.tensor.transpose(x_bank[:, b, :], x_bf[:, b : b + 1].to_broadcast([P, P]), identity_bf[:])
-        x_rows = keep.tile([P, BATCHES, P], F32)
-        nc.vector.tensor_copy(out=x_rows[:], in_=x_bank[:])
-
         x_pair = keep.tile([P, BATCHES, P], BF16)
         nc.vector.memset(x_pair[:], 0.0)
         nc.vector.memset(x_pair[ONES_PARTITION : ONES_PARTITION + 1, :, :], 1.0)
@@ -84,13 +77,39 @@ def tile_softembedding_k_kernel(tc, input_numeric, proj_w, proj_b, emb_table, ou
         w_view = proj_w.rearrange("(q i n) o -> o i q n", i=TENSOR_OF, n=K_PASS)
         b_view = proj_b.rearrange("(o q i n) -> o i q n", o=1, i=TENSOR_OF, n=K_PASS)
         proj_pair = []
-        for slot, residue in enumerate(TENSOR_RESIDUES):
+        for slot in range(TENSOR_SHARE):
             pair = keep.tile([P, PASSES // TENSOR_OF, K_PASS], BF16, name="proj_pair%d" % slot)
             zero_engine = nc.gpsimd if slot == TENSOR_SHARE - 1 else nc.vector
             zero_engine.memset(pair[:].bitcast(F32), 0.0)
-            nc.sync.dma_start(out=pair[0:1, :, :], in_=w_view[:, residue, :, :])
-            nc.sync.dma_start(out=pair[ONES_PARTITION : ONES_PARTITION + 1, :, :], in_=b_view[:, residue, :, :])
             proj_pair.append(pair)
+
+        last_pair = keep.tile([P, K_PASS], BF16)
+        nc.gpsimd.memset(last_pair[:].bitcast(F32), 0.0)
+
+        def load_last_pair():
+            first = VOCAB - K_PASS
+            nc.sync.dma_start(out=last_pair[0:1, :], in_=proj_w[first:VOCAB, :].rearrange("n o -> o n"))
+            nc.sync.dma_start(
+                out=last_pair[ONES_PARTITION : ONES_PARTITION + 1, :], in_=proj_b[first:VOCAB].unsqueeze(0)
+            )
+
+        def load_pair(slot):
+            residue = TENSOR_RESIDUES[slot]
+            nc.sync.dma_start(out=proj_pair[slot][0:1, :, :], in_=w_view[:, residue, :, :])
+            nc.sync.dma_start(
+                out=proj_pair[slot][ONES_PARTITION : ONES_PARTITION + 1, :, :], in_=b_view[:, residue, :, :]
+            )
+
+        head_bank = psum_out.tile([P, 2, P], BF16, tag="row_acc")
+        nc.tensor.transpose(head_bank[:, 0, :], proj_loaded[:, 0, :], identity_bf[:])
+        nc.tensor.transpose(head_bank[:, 1, :], proj_loaded[:, 1, :], identity_bf[:])
+        x_bank = psum_turn.tile([P, BATCHES, P], BF16, tag="turn_bank")
+        for b in range(BATCHES):
+            nc.tensor.transpose(x_bank[:, b, :], x_bf[:, b : b + 1].to_broadcast([P, P]), identity_bf[:])
+        proj_cols = keep.tile([P, 2, P], F32)
+        nc.vector.tensor_copy(out=proj_cols[:], in_=head_bank[:])
+        x_rows = keep.tile([P, BATCHES, P], F32)
+        nc.vector.tensor_copy(out=x_rows[:], in_=x_bank[:])
 
         table_codes = keep.tile([P, PASSES, DIM], U32, align_bytes=64)
         table_scales = keep.tile([P, PASSES // PLANES, DIM], U8, align_bytes=64)
@@ -146,8 +165,17 @@ def tile_softembedding_k_kernel(tc, input_numeric, proj_w, proj_b, emb_table, ou
         inverse = {}
         row_scale = {}
 
+        def last_by_tensor(q):
+            return q % PASSES == PASSES - 1 and q < LAST_PASS_ROWS * PASSES
+
         def by_tensor(q):
-            return q % TENSOR_OF in TENSOR_RESIDUES
+            return q % TENSOR_OF in TENSOR_RESIDUES or last_by_tensor(q)
+
+        def projection(q):
+            if last_by_tensor(q):
+                return last_pair[:]
+            i = q % PASSES
+            return proj_pair[TENSOR_RESIDUES.index(i % TENSOR_OF)][:, i // TENSOR_OF, :]
 
         def columns(q, scalar_share):
             b, i = divmod(q, PASSES)
@@ -192,7 +220,7 @@ def tile_softembedding_k_kernel(tc, input_numeric, proj_w, proj_b, emb_table, ou
                 nc.tensor.matmul(
                     out=logit_bank[:],
                     lhsT=x_pair[:, b, :],
-                    rhs=proj_pair[TENSOR_RESIDUES.index(i % TENSOR_OF)][:, i // TENSOR_OF, :],
+                    rhs=projection(q),
                     start=True,
                     stop=True,
                 )
@@ -295,7 +323,16 @@ def tile_softembedding_k_kernel(tc, input_numeric, proj_w, proj_b, emb_table, ou
             source = exps[k][:].rearrange("s c n -> s (c n)")
             scale = row_scale[b][:, j : j + 1]
             if one is None:
-                nc.vector.tensor_scalar(out=target, in0=source, scalar1=scale, scalar2=None, op0=ALU.mult)
+                nc.vector.tensor_scalar(
+                    out=target[:, :VECTOR_WEIGHTS],
+                    in0=source[:, :VECTOR_WEIGHTS],
+                    scalar1=scale,
+                    scalar2=None,
+                    op0=ALU.mult,
+                )
+                nc.scalar.activation(
+                    out=target[:, VECTOR_WEIGHTS:], in_=source[:, VECTOR_WEIGHTS:], func=ACT.Copy, scale=scale
+                )
             else:
                 nc.gpsimd.tensor_scalar(
                     out=target, in0=source, scalar1=scale, scalar2=one[:, 0:1], op0=ALU.mult, op1=ALU.mult
@@ -362,107 +399,131 @@ def tile_softembedding_k_kernel(tc, input_numeric, proj_w, proj_b, emb_table, ou
         def slices_of(k):
             return range(STEP * k, STEP * (k + 1))
 
-        with tc.manual_schedule():
-            with tc.tile_pool(name="table_stage", bufs=1) as table_stage:
-                for g in [2, 0, 1] + list(range(3, LOAD_AHEAD)):
-                    load_table(table_stage, g)
-                for q in slices_of(0):
-                    columns(q, 0)
-                for q in fill_order(0):
+        with tc.tile_pool(name="table_stage", bufs=1) as table_stage:
+            load_table(table_stage, 2)
+            load_pair(0)
+            load_pair(1)
+            load_table(table_stage, 0)
+            load_pair(2)
+            for g in [1] + list(range(3, LOAD_AHEAD)):
+                load_table(table_stage, g)
+            load_last_pair()
+            for q in slices_of(0):
+                columns(q, 0)
+            for q in fill_order(0):
+                logits(q)
+            for k in range(ROW_STEPS):
+                passes = slices_of(k)
+                one = stats.tile([P, 1], F32)
+                nc.vector.memset(one[:], 1.0)
+                regroup_table(table_stage, passes[0], "gpsimd", one)
+                collect(k)
+                if k == 0:
+                    regroup_table(table_stage, passes[2], "scalar", None)
+                for q in slices_of(k + 1):
+                    columns(q, HEAD_SCALAR_COLUMNS)
+                for q in slices_of(k + 1):
+                    scalar_columns(q, HEAD_SCALAR_COLUMNS)
+                maximum(k)
+                exponentials(k)
+                for q in fill_order(k + 1):
                     logits(q)
-                for k in range(ROW_STEPS):
-                    passes = slices_of(k)
+                if k >= 1:
+                    for g in slices_of(k - 1):
+                        quantise_table(g)
+                regroup_table(table_stage, passes[1], "vector", None)
+                if k >= 1:
+                    regroup_table(table_stage, passes[2], "scalar", None)
+                regroup_table(table_stage, passes[3], "scalar", None)
+                for g in passes:
+                    if g + LOAD_AHEAD < PASSES:
+                        load_table(table_stage, g + LOAD_AHEAD)
+            for g in slices_of(ROW_STEPS - 1):
+                quantise_table(g)
+
+        with tc.tile_pool(name="weight_stage", bufs=2) as stage:
+            last = STEPS - 1
+
+            def normalise_step(k, release):
+                weight_tile(stage, k)
+                one = None
+                if release:
                     one = stats.tile([P, 1], F32)
                     nc.vector.memset(one[:], 1.0)
-                    regroup_table(table_stage, passes[0], "gpsimd", one)
-                    collect(k)
-                    if k == 0:
-                        regroup_table(table_stage, passes[2], "scalar", None)
-                    for q in slices_of(k + 1):
-                        columns(q, HEAD_SCALAR_COLUMNS)
-                    for q in slices_of(k + 1):
-                        scalar_columns(q, HEAD_SCALAR_COLUMNS)
-                    maximum(k)
-                    exponentials(k)
-                    for q in fill_order(k + 1):
-                        logits(q)
-                    if k >= 1:
-                        for g in slices_of(k - 1):
-                            quantise_table(g)
-                    regroup_table(table_stage, passes[1], "vector", None)
-                    if k >= 1:
-                        regroup_table(table_stage, passes[2], "scalar", None)
-                    regroup_table(table_stage, passes[3], "scalar", None)
-                    for g in passes:
-                        if g + LOAD_AHEAD < PASSES:
-                            load_table(table_stage, g + LOAD_AHEAD)
-                for g in slices_of(ROW_STEPS - 1):
-                    quantise_table(g)
+                normalise(k, one)
 
-            with tc.tile_pool(name="weight_stage", bufs=2) as stage:
-                last = STEPS - 1
-                for k in range(ROW_STEPS, last + QUANTISE_LAG):
-                    row_ends = k % ROW_STEPS == 0 and k <= STEPS
-                    b = k // ROW_STEPS - 1
-                    soft = k < STEPS
-                    kw = k - WEIGHT_LAG
-                    kt = k - TURN_LAG
-                    kq = k - QUANTISE_LAG
-                    km = k - MULTIPLY_LAG
-                    has_next = k + 1 < STEPS
-                    if 0 <= kw < STEPS:
-                        weight_tile(stage, kw)
-                        one = None
-                        if k <= STEPS:
-                            one = stats.tile([P, 1], F32)
-                            nc.vector.memset(one[:], 1.0)
-                        normalise(kw, one)
-                    if row_ends:
-                        row_top(b)
-                    if 0 <= kt < STEPS:
-                        turn(2 * kt)
-                        turn(2 * kt + 1)
-                    if kt == last:
-                        code_tiles(stage, last)
-                    if 0 <= km < STEPS:
-                        multiply(km, (0, 1))
-                    if soft:
-                        collect(k)
-                    if row_ends:
-                        row_factors(b)
-                    if 0 <= kt < STEPS:
-                        regroup(stage, 2 * kt)
-                    tasks = [row_total, row_inverse, row_scales] if row_ends else []
-                    if has_next:
-                        for q in slices_of(k + 1):
-                            if tasks:
-                                tasks.pop(0)(b)
-                            columns(q, 1 + q % 2)
-                        for q in slices_of(k + 1):
-                            scalar_columns(q, 1 + q % 2)
-                    for task in tasks:
-                        task(b)
-                    if 0 <= kt < STEPS:
-                        regroup(stage, 2 * kt + 1)
-                    if soft:
-                        maximum(k)
-                        exponentials(k)
-                    fills = fill_order(k + 1) if has_next else []
-                    for q in fills[:2]:
-                        logits(q)
-                    if 0 <= km < STEPS:
-                        multiply(km, (2, 3))
-                        if km % ROW_STEPS == ROW_STEPS - 1:
-                            store(stage, km // ROW_STEPS)
-                    for q in fills[2:]:
-                        logits(q)
-                    if 0 <= kq < last:
-                        code_tiles(stage, kq)
-                        quantise(kq, 0, STEP)
-                    if kt == last:
-                        quantise(last, 0, PAIR)
-                        quantise(last, PAIR, STEP)
-                multiply(last - 1, range(STEP))
-                multiply(last, (0, 1))
-                multiply(last, (2, 3))
-                store(stage, BATCHES - 1)
+            def turn_step(k):
+                if k >= 0:
+                    turn(2 * k)
+                    turn(2 * k + 1)
+
+            def multiply_half(k, half):
+                if k >= 0:
+                    multiply(k, (2 * half, 2 * half + 1))
+                    if half == 1 and k % ROW_STEPS == ROW_STEPS - 1:
+                        store(stage, k // ROW_STEPS)
+
+            def regroup_half(k, half):
+                if k >= 0:
+                    regroup(stage, 2 * k + half)
+
+            def quantise_step(k):
+                if k >= 0:
+                    code_tiles(stage, k)
+                    quantise(k, 0, STEP)
+
+            for k in range(ROW_STEPS, STEPS):
+                row_ends = k % ROW_STEPS == 0
+                b = k // ROW_STEPS - 1
+                kw = k - WEIGHT_LAG
+                if kw >= 0:
+                    normalise_step(kw, True)
+                if row_ends:
+                    row_top(b)
+                turn_step(kw - 1)
+                multiply_half(kw - 3, 0)
+                collect(k)
+                if row_ends:
+                    row_factors(b)
+                regroup_half(kw - 1, 0)
+                tasks = [row_total, row_inverse, row_scales] if row_ends else []
+                fills = fill_order(k + 1) if k < last else []
+                if k < last:
+                    for q in slices_of(k + 1):
+                        if tasks:
+                            tasks.pop(0)(b)
+                        columns(q, 1 + q % 2)
+                    for q in slices_of(k + 1):
+                        scalar_columns(q, 1 + q % 2)
+                regroup_half(kw - 1, 1)
+                maximum(k)
+                exponentials(k)
+                for q in fills[:2]:
+                    logits(q)
+                multiply_half(kw - 3, 1)
+                for q in fills[2:]:
+                    logits(q)
+                quantise_step(kw - 2)
+
+            for kw in range(STEPS - WEIGHT_LAG, STEPS + 1):
+                if kw == STEPS - ROW_STEPS:
+                    row_total(BATCHES - 1)
+                    row_inverse(BATCHES - 1)
+                    row_scales(BATCHES - 1)
+                if kw <= last:
+                    normalise_step(kw, kw < STEPS - ROW_STEPS)
+                if kw == STEPS - WEIGHT_LAG:
+                    row_top(BATCHES - 1)
+                    row_factors(BATCHES - 1)
+                turn_step(kw - 1)
+                multiply_half(kw - 3, 0)
+                regroup_half(kw - 1, 0)
+                regroup_half(kw - 1, 1)
+                multiply_half(kw - 3, 1)
+                quantise_step(kw - 2)
+            code_tiles(stage, last)
+            for half in range(2):
+                quantise(last, 2 * half, 2 * half + 2)
+            for k in (last - 1, last):
+                for half in range(2):
+                    multiply_half(k, half)

from contextlib import ExitStack

import concourse.mybir as mybir
from concourse.masks import make_identity

F32 = mybir.dt.float32
BF16 = mybir.dt.bfloat16
U32 = mybir.dt.uint32
U8 = mybir.dt.uint8
FP8X4 = mybir.dt.float8_e4m3fn_x4
ALU = mybir.AluOpType
ACT = mybir.ActivationFunctionType
AXIS = mybir.AxisListType

P = 128
BATCHES = 4
VOCAB = 16384
DIM = 512
PACK = 4
K_PASS = P * PACK
PASSES = VOCAB // K_PASS
TOTAL = BATCHES * PASSES
COLS = K_PASS // P
PAIR = 2
PLANES = 4
PLANE_ROWS = 4
RUN = 4
TENSOR_SHARE = 3
TENSOR_OF = 8
TENSOR_RESIDUES = [i for i in range(TENSOR_OF) if TENSOR_SHARE * i % TENSOR_OF < TENSOR_SHARE]
LAST_PASS_ROWS = 3
ONES_PARTITION = 32
STEP = 4
STEPS = TOTAL // STEP
ROW_STEPS = PASSES // STEP
LOAD_AHEAD = 8
WEIGHT_LAG = ROW_STEPS + 1
TURN_LAG = WEIGHT_LAG + 1
QUANTISE_LAG = WEIGHT_LAG + 2
MULTIPLY_LAG = WEIGHT_LAG + 3
EXP_BUFS = WEIGHT_LAG + 1
VECTOR_WEIGHTS = 1792
HEAD_SCALAR_COLUMNS = 1

FLOPS = 2 * BATCHES * P * VOCAB * DIM


def tile_softembedding_k_kernel(tc, input_numeric, proj_w, proj_b, emb_table, out):
    nc = tc.nc
    with ExitStack() as ctx:
        keep = ctx.enter_context(tc.tile_pool(name="keep", bufs=1))
        exp_pool = ctx.enter_context(tc.tile_pool(name="exp_pool", bufs=EXP_BUFS))
        logit_cols = ctx.enter_context(tc.tile_pool(name="logit_cols", bufs=5))
        stats = ctx.enter_context(tc.tile_pool(name="stats", bufs=2))
        psum_logit = ctx.enter_context(tc.psum_pool(name="psum_logit", bufs=4))
        psum_turn = ctx.enter_context(tc.psum_pool(name="psum_turn", bufs=2))
        psum_out = ctx.enter_context(tc.psum_pool(name="psum_out", bufs=2))

        ctx.enter_context(tc.manual_schedule())

        x_bf = keep.tile([P, BATCHES], BF16)
        with nc.allow_non_contiguous_dma(reason="512 scalars, one token to a partition"):
            nc.sync.dma_start(out=x_bf[:], in_=input_numeric.rearrange("b s o -> s (b o)"))
        proj_loaded = keep.tile([P, 2, P], BF16)
        nc.sync.dma_start(out=proj_loaded[:, 0, :], in_=proj_w.rearrange("(a p) o -> a (p o)", p=P))
        nc.sync.dma_start(out=proj_loaded[:, 1, :], in_=proj_b.rearrange("(a p) -> a p", p=P))

        identity_bf = keep.tile([P, P], BF16)
        make_identity(nc, identity_bf[:])
        identity = keep.tile([P, P], F32)
        make_identity(nc, identity[:])

        x_pair = keep.tile([P, BATCHES, P], BF16)
        nc.vector.memset(x_pair[:], 0.0)
        nc.vector.memset(x_pair[ONES_PARTITION : ONES_PARTITION + 1, :, :], 1.0)
        nc.sync.dma_start(out=x_pair[0:1, :, :], in_=input_numeric.rearrange("b s o -> o b s"))
        w_view = proj_w.rearrange("(q i n) o -> o i q n", i=TENSOR_OF, n=K_PASS)
        b_view = proj_b.rearrange("(o q i n) -> o i q n", o=1, i=TENSOR_OF, n=K_PASS)
        proj_pair = []
        for slot in range(TENSOR_SHARE):
            pair = keep.tile([P, PASSES // TENSOR_OF, K_PASS], BF16, name="proj_pair%d" % slot)
            zero_engine = nc.gpsimd if slot == TENSOR_SHARE - 1 else nc.vector
            zero_engine.memset(pair[:].bitcast(F32), 0.0)
            proj_pair.append(pair)

        last_pair = keep.tile([P, K_PASS], BF16)
        nc.gpsimd.memset(last_pair[:].bitcast(F32), 0.0)

        def load_last_pair():
            first = VOCAB - K_PASS
            nc.sync.dma_start(out=last_pair[0:1, :], in_=proj_w[first:VOCAB, :].rearrange("n o -> o n"))
            nc.sync.dma_start(
                out=last_pair[ONES_PARTITION : ONES_PARTITION + 1, :], in_=proj_b[first:VOCAB].unsqueeze(0)
            )

        def load_pair(slot):
            residue = TENSOR_RESIDUES[slot]
            nc.sync.dma_start(out=proj_pair[slot][0:1, :, :], in_=w_view[:, residue, :, :])
            nc.sync.dma_start(
                out=proj_pair[slot][ONES_PARTITION : ONES_PARTITION + 1, :, :], in_=b_view[:, residue, :, :]
            )

        head_bank = psum_out.tile([P, 2, P], BF16, tag="row_acc")
        nc.tensor.transpose(head_bank[:, 0, :], proj_loaded[:, 0, :], identity_bf[:])
        nc.tensor.transpose(head_bank[:, 1, :], proj_loaded[:, 1, :], identity_bf[:])
        x_bank = psum_turn.tile([P, BATCHES, P], BF16, tag="turn_bank")
        for b in range(BATCHES):
            nc.tensor.transpose(x_bank[:, b, :], x_bf[:, b : b + 1].to_broadcast([P, P]), identity_bf[:])
        proj_cols = keep.tile([P, 2, P], F32)
        nc.vector.tensor_copy(out=proj_cols[:], in_=head_bank[:])
        x_rows = keep.tile([P, BATCHES, P], F32)
        nc.vector.tensor_copy(out=x_rows[:], in_=x_bank[:])

        table_codes = keep.tile([P, PASSES, DIM], U32, align_bytes=64)
        table_scales = keep.tile([P, PASSES // PLANES, DIM], U8, align_bytes=64)

        def table_plane(g):
            return table_scales[PLANE_ROWS * (g % PLANES) : P, g // PLANES, :]

        table_rows = {}
        table_grouped = {}

        def load_table(stage, g):
            pass_rows = stage.tile([P, PACK, DIM], BF16, bufs=LOAD_AHEAD)
            nc.sync.dma_start(
                out=pass_rows[:],
                in_=emb_table[g * K_PASS : (g + 1) * K_PASS, :].rearrange("(p t) d -> p t d", t=PACK),
            )
            table_rows[g] = pass_rows

        def regroup_table(stage, g, engine, one):
            pass_grouped = stage.tile([P, DIM, PACK], BF16, align_bytes=64, bufs=6)
            dst = pass_grouped[:].rearrange("p (r i) t -> p r t i", i=RUN)
            src = table_rows[g][:].rearrange("p t (r i) -> p r t i", i=RUN)
            table_grouped[g] = pass_grouped
            if engine == "gpsimd":
                nc.gpsimd.tensor_scalar(
                    out=pass_grouped[:],
                    in0=table_rows[g][:].rearrange("p t d -> p d t"),
                    scalar1=one[:, 0:1],
                    scalar2=0.0,
                    op0=ALU.mult,
                    op1=ALU.add,
                )
            elif engine == "vector":
                nc.vector.tensor_copy(out=dst, in_=src)
            else:
                nc.scalar.copy(out=dst, in_=src)

        def quantise_table(g):
            nc.vector.quantize_mx(
                out=table_codes[:, g, :].bitcast(FP8X4),
                scales=table_plane(g),
                in_=table_grouped[g][:].rearrange("p d t -> p (d t)"),
            )

        slice_cols = {}
        slice_max = {}
        logit_banks = {}
        exps = {}
        neg_max = {}
        part_sum = {}
        neg_top = {}
        factors = {}
        inverse = {}
        row_scale = {}

        def last_by_tensor(q):
            return q % PASSES == PASSES - 1 and q < LAST_PASS_ROWS * PASSES

        def by_tensor(q):
            return q % TENSOR_OF in TENSOR_RESIDUES or last_by_tensor(q)

        def projection(q):
            if last_by_tensor(q):
                return last_pair[:]
            i = q % PASSES
            return proj_pair[TENSOR_RESIDUES.index(i % TENSOR_OF)][:, i // TENSOR_OF, :]

        def columns(q, scalar_share):
            b, i = divmod(q, PASSES)
            if i == 0:
                row_neg_max = stats.tile([P, ROW_STEPS], F32)
                row_part_sum = stats.tile([P, ROW_STEPS], F32)
                neg_max[b] = row_neg_max
                part_sum[b] = row_part_sum
            if by_tensor(q):
                return
            cols = logit_cols.tile([P, COLS, P], F32)
            slice_cols[q] = cols
            for c in range(COLS - scalar_share):
                a = COLS * i + c
                nc.vector.tensor_scalar(
                    out=cols[:, c, :],
                    in0=x_rows[:, b, :],
                    scalar1=proj_cols[:, 0, a : a + 1],
                    scalar2=proj_cols[:, 1, a : a + 1],
                    op0=ALU.mult,
                    op1=ALU.add,
                )

        def scalar_columns(q, scalar_share):
            b, i = divmod(q, PASSES)
            if by_tensor(q):
                return
            for c in range(COLS - scalar_share, COLS):
                a = COLS * i + c
                nc.scalar.activation(
                    out=slice_cols[q][:, c, :],
                    in_=x_rows[:, b, :],
                    func=ACT.Identity,
                    scale=proj_cols[:, 0, a : a + 1],
                    bias=proj_cols[:, 1, a : a + 1],
                )

        def logits(q):
            b, i = divmod(q, PASSES)
            logit_bank = psum_logit.tile([P, K_PASS], F32)
            if by_tensor(q):
                nc.tensor.matmul(
                    out=logit_bank[:],
                    lhsT=x_pair[:, b, :],
                    rhs=projection(q),
                    start=True,
                    stop=True,
                )
            else:
                for c in range(COLS):
                    nc.tensor.transpose(logit_bank[:, c * P : (c + 1) * P], slice_cols[q][:, c, :], identity[:])
            logit_banks[q] = logit_bank

        def fill_order(k):
            slices = range(STEP * k, STEP * (k + 1))
            return [q for q in slices if by_tensor(q)] + [q for q in slices if not by_tensor(q)]

        def collect(k):
            step_exps = exp_pool.tile([P, STEP, K_PASS], F32)
            step_max = stats.tile([P, STEP], F32)
            for q in fill_order(k):
                c = q - STEP * k
                nc.vector.tensor_scalar(
                    out=step_exps[:, c, :].rearrange("s (u p e) -> s u p e", u=2, e=2),
                    in0=logit_banks[q][:].rearrange("s (p u e) -> s u p e", u=2, e=2),
                    scalar1=0.0,
                    scalar2=None,
                    op0=ALU.add,
                    op1=ALU.max,
                    accum_out=step_max[:, c : c + 1],
                )
            exps[k] = step_exps
            slice_max[k] = step_max

        def maximum(k):
            b, j = divmod(k, ROW_STEPS)
            nc.vector.tensor_reduce(
                out=neg_max[b][:, j : j + 1], in_=slice_max[k][:], axis=AXIS.X, op=ALU.max, negate=True
            )

        def exponentials(k):
            b, j = divmod(k, ROW_STEPS)
            logits_and_exps = exps[k][:].rearrange("s c n -> s (c n)")
            nc.scalar.activation(
                out=logits_and_exps,
                in_=logits_and_exps,
                func=ACT.Exp,
                bias=neg_max[b][:, j : j + 1],
                scale=1.0,
                accum_out=part_sum[b][:, j : j + 1],
            )

        def row_top(b):
            top = stats.tile([P, 1], F32)
            nc.vector.tensor_reduce(out=top[:], in_=neg_max[b][:], axis=AXIS.X, op=ALU.min)
            neg_top[b] = top

        def row_factors(b):
            factor = stats.tile([P, ROW_STEPS], F32)
            nc.scalar.activation(
                out=factor[:], in_=neg_max[b][:], func=ACT.Exp, bias=neg_top[b][:, 0:1], scale=-1.0
            )
            factors[b] = factor

        def row_total(b):
            weighted = stats.tile([P, ROW_STEPS], F32)
            total = stats.tile([P, 1], F32)
            nc.vector.scalar_tensor_tensor(
                out=weighted[:],
                in0=factors[b][:],
                scalar=1.0,
                in1=part_sum[b][:],
                op0=ALU.mult,
                op1=ALU.mult,
                accum_out=total[:],
            )
            inverse[b] = total

        def row_inverse(b):
            inv_total = stats.tile([P, 1], F32)
            nc.vector.reciprocal(out=inv_total[:], in_=inverse[b][:])
            inverse[b] = inv_total

        def row_scales(b):
            scales = stats.tile([P, ROW_STEPS], F32)
            nc.vector.tensor_scalar(
                out=scales[:], in0=factors[b][:], scalar1=inverse[b][:, 0:1], scalar2=None, op0=ALU.mult
            )
            row_scale[b] = scales

        weights = {}
        turned = {}
        weight_grouped = {}
        weight_codes = {}
        weight_scales = {}
        acc = {}

        def weight_tile(stage, k):
            step_weights = stage.tile([P, STEP, K_PASS], BF16)
            weights[k] = step_weights

        def normalise(k, one):
            b, j = divmod(k, ROW_STEPS)
            target = weights[k][:].rearrange("s c n -> s (c n)")
            source = exps[k][:].rearrange("s c n -> s (c n)")
            scale = row_scale[b][:, j : j + 1]
            if one is None:
                nc.vector.tensor_scalar(
                    out=target[:, :VECTOR_WEIGHTS],
                    in0=source[:, :VECTOR_WEIGHTS],
                    scalar1=scale,
                    scalar2=None,
                    op0=ALU.mult,
                )
                nc.scalar.activation(
                    out=target[:, VECTOR_WEIGHTS:], in_=source[:, VECTOR_WEIGHTS:], func=ACT.Copy, scale=scale
                )
            else:
                nc.gpsimd.tensor_scalar(
                    out=target, in0=source, scalar1=scale, scalar2=one[:, 0:1], op0=ALU.mult, op1=ALU.mult
                )

        def turn(pair):
            k, half = divmod(pair, STEP // PAIR)
            words = weights[k][:].rearrange("s c n -> s (c n)").bitcast(F32)
            turned_bank = psum_turn.tile([P, PAIR, 2, P], F32, tag="turn_bank")
            for c in range(PAIR):
                for u in range(2):
                    first = (2 * (PAIR * half + c) + u) * P
                    nc.tensor.transpose(turned_bank[:, c, u, :], words[:, first : first + P], identity[:])
            turned[pair] = turned_bank

        def regroup(stage, pair):
            k, half = divmod(pair, STEP // PAIR)
            if half == 0:
                step_grouped = stage.tile([P, STEP, P, PACK], BF16, align_bytes=64)
                weight_grouped[k] = step_grouped
            words = weight_grouped[k][:].bitcast(F32)
            nc.scalar.copy(
                out=words[:, PAIR * half : PAIR * (half + 1), :, :],
                in_=turned[pair][:].rearrange("p c u s -> p c s u"),
            )

        def code_tiles(stage, k):
            step_codes = stage.tile([P, STEP * P], U32, align_bytes=64)
            step_planes = stage.tile([P, STEP * P], U8, align_bytes=64)
            weight_codes[k] = step_codes
            weight_scales[k] = step_planes

        def quantise(k, first, last):
            tokens = slice(first * P, last * P)
            nc.vector.quantize_mx(
                out=weight_codes[k][:, tokens].bitcast(FP8X4),
                scales=weight_scales[k][:, tokens],
                in_=weight_grouped[k][:, first:last, :, :].rearrange("p c s t -> p (c s t)"),
            )

        def multiply(k, part):
            b, j = divmod(k, ROW_STEPS)
            if j == 0 and part[0] == 0:
                row_acc = psum_out.tile([P, DIM], F32)
                acc[b] = row_acc
            for c in part:
                g = j * STEP + c
                tokens = slice(c * P, (c + 1) * P)
                nc.tensor.matmul_mx(
                    out=acc[b][:],
                    lhsT=weight_codes[k][:, tokens].bitcast(FP8X4),
                    lhsT_scale=weight_scales[k][:, tokens],
                    rhs=table_codes[:, g, :].bitcast(FP8X4),
                    rhs_scale=table_plane(g),
                    start=(g == 0),
                    stop=(g == PASSES - 1),
                )

        def store(stage, b):
            result = stage.tile([P, DIM], F32, bufs=1)
            nc.scalar.copy(out=result[:], in_=acc[b][:])
            nc.sync.dma_start(out=out[b], in_=result[:])

        def slices_of(k):
            return range(STEP * k, STEP * (k + 1))

        with tc.tile_pool(name="table_stage", bufs=1) as table_stage:
            load_table(table_stage, 2)
            load_pair(0)
            load_pair(1)
            load_table(table_stage, 0)
            load_pair(2)
            for g in [1] + list(range(3, LOAD_AHEAD)):
                load_table(table_stage, g)
            load_last_pair()
            for q in slices_of(0):
                columns(q, 0)
            for q in fill_order(0):
                logits(q)
            for k in range(ROW_STEPS):
                passes = slices_of(k)
                one = stats.tile([P, 1], F32)
                nc.vector.memset(one[:], 1.0)
                regroup_table(table_stage, passes[0], "gpsimd", one)
                collect(k)
                if k == 0:
                    regroup_table(table_stage, passes[2], "scalar", None)
                for q in slices_of(k + 1):
                    columns(q, HEAD_SCALAR_COLUMNS)
                for q in slices_of(k + 1):
                    scalar_columns(q, HEAD_SCALAR_COLUMNS)
                maximum(k)
                exponentials(k)
                for q in fill_order(k + 1):
                    logits(q)
                if k >= 1:
                    for g in slices_of(k - 1):
                        quantise_table(g)
                regroup_table(table_stage, passes[1], "vector", None)
                if k >= 1:
                    regroup_table(table_stage, passes[2], "scalar", None)
                regroup_table(table_stage, passes[3], "scalar", None)
                for g in passes:
                    if g + LOAD_AHEAD < PASSES:
                        load_table(table_stage, g + LOAD_AHEAD)
            for g in slices_of(ROW_STEPS - 1):
                quantise_table(g)

        with tc.tile_pool(name="weight_stage", bufs=2) as stage:
            last = STEPS - 1

            def normalise_step(k, release):
                weight_tile(stage, k)
                one = None
                if release:
                    one = stats.tile([P, 1], F32)
                    nc.vector.memset(one[:], 1.0)
                normalise(k, one)

            def turn_step(k):
                if k >= 0:
                    turn(2 * k)
                    turn(2 * k + 1)

            def multiply_half(k, half):
                if k >= 0:
                    multiply(k, (2 * half, 2 * half + 1))
                    if half == 1 and k % ROW_STEPS == ROW_STEPS - 1:
                        store(stage, k // ROW_STEPS)

            def regroup_half(k, half):
                if k >= 0:
                    regroup(stage, 2 * k + half)

            def quantise_step(k):
                if k >= 0:
                    code_tiles(stage, k)
                    quantise(k, 0, STEP)

            for k in range(ROW_STEPS, STEPS):
                row_ends = k % ROW_STEPS == 0
                b = k // ROW_STEPS - 1
                kw = k - WEIGHT_LAG
                if kw >= 0:
                    normalise_step(kw, True)
                if row_ends:
                    row_top(b)
                turn_step(kw - 1)
                multiply_half(kw - 3, 0)
                collect(k)
                if row_ends:
                    row_factors(b)
                regroup_half(kw - 1, 0)
                tasks = [row_total, row_inverse, row_scales] if row_ends else []
                fills = fill_order(k + 1) if k < last else []
                if k < last:
                    for q in slices_of(k + 1):
                        if tasks:
                            tasks.pop(0)(b)
                        columns(q, 1 + q % 2)
                    for q in slices_of(k + 1):
                        scalar_columns(q, 1 + q % 2)
                regroup_half(kw - 1, 1)
                maximum(k)
                exponentials(k)
                for q in fills[:2]:
                    logits(q)
                multiply_half(kw - 3, 1)
                for q in fills[2:]:
                    logits(q)
                quantise_step(kw - 2)

            for kw in range(STEPS - WEIGHT_LAG, STEPS + 1):
                if kw == STEPS - ROW_STEPS:
                    row_total(BATCHES - 1)
                    row_inverse(BATCHES - 1)
                    row_scales(BATCHES - 1)
                if kw <= last:
                    normalise_step(kw, kw < STEPS - ROW_STEPS)
                if kw == STEPS - WEIGHT_LAG:
                    row_top(BATCHES - 1)
                    row_factors(BATCHES - 1)
                turn_step(kw - 1)
                multiply_half(kw - 3, 0)
                regroup_half(kw - 1, 0)
                regroup_half(kw - 1, 1)
                multiply_half(kw - 3, 1)
                quantise_step(kw - 2)
            code_tiles(stage, last)
            for half in range(2):
                quantise(last, 2 * half, 2 * half + 2)
            for k in (last - 1, last):
                for half in range(2):
                    multiply_half(k, half)
